import numpy as np
import ml_dtypes


def mxq(x, axis, fmt="e4m3"):
    dtype, down = {"e4m3": (ml_dtypes.float8_e4m3fn, 7), "e5m2": (ml_dtypes.float8_e5m2, 14)}[fmt]
    v = np.moveaxis(np.asarray(x, np.float32).astype(ml_dtypes.bfloat16).astype(np.float64), axis, -1)
    blocks = v.reshape(v.shape[:-1] + (-1, 32))
    amax = np.abs(blocks).max(-1, keepdims=True)
    byte = np.maximum(np.where(amax > 0, np.frexp(amax)[1] - 1 + 127, 0) - down, 1)
    scale = np.exp2(byte - 127.0)
    codes = (blocks / scale).astype(np.float32).astype(dtype).astype(np.float64)
    return np.moveaxis((codes * scale).reshape(v.shape), -1, axis)


WIDE = False


def mx_kscale(k):
    if not WIDE:
        return np.ones(k)
    levels = np.array([10, -10, 5, -5, 0])
    a = np.random.permutation(np.resize(levels, k // 512 * 4)).reshape(k // 512, 4)
    idx = np.arange(k)
    return np.exp2(a[idx // 512, idx % 128 // 32])


BF16 = ml_dtypes.bfloat16


def bf(x):
    return np.asarray(x, np.float32).astype(BF16)


def f64(x):
    return np.asarray(x).astype(np.float64)


B, S, DI, DO = 4, 1024, 1024, 1024
R = B * S
LN_EPS = 1e-5


def ste_sign(w):
    return np.where(w >= 0, 1.0, -1.0)


def setup_inputs():
    r = np.asarray(mx_kscale(DI), np.float64)[np.arange(R) * DI // R]
    return {"x": bf(np.random.standard_normal((B, S, DI)) * r.reshape(B, S, 1)),
            "weight": bf(np.random.standard_normal((DO, DI)) * 0.02),
            "in_channel_scale": bf(np.random.uniform(0.5, 1.5, DI) / np.sqrt(DI)),
            "out_channel_scale": bf(np.random.uniform(0.5, 1.5, DO) / r.min()),
            "bias": bf(np.random.standard_normal(DO) * 0.3),
            "ln_gamma": bf(1.0 + 0.1 * np.random.standard_normal(DO)),
            "ln_beta": bf(0.1 * np.random.standard_normal(DO))}


def reference(x, weight, in_channel_scale, out_channel_scale, bias, ln_gamma, ln_beta):
    x = f64(x)
    orig_shape = x.shape
    xf = x.reshape(-1, orig_shape[-1])
    w_bin = ste_sign(f64(weight))
    xs = xf * f64(in_channel_scale)
    h = (mxq(xs, 1, "e4m3") @ mxq(w_bin, 1, "e4m3").T) * f64(out_channel_scale)
    h = h + f64(bias)
    mu = np.mean(h, axis=-1, keepdims=True)
    var = np.mean(np.square(h - mu), axis=-1, keepdims=True)
    h = (h - mu) / np.sqrt(var + LN_EPS) * f64(ln_gamma) + f64(ln_beta)
    return h.reshape(*orig_shape[:-1], weight.shape[0])

@@ -1,0 +1,299 @@
+from contextlib import ExitStack
+
+import concourse.mybir as mybir
+from concourse.masks import make_identity
+
+F32 = mybir.dt.float32
+BF16 = mybir.dt.bfloat16
+U32 = mybir.dt.uint32
+U8 = mybir.dt.uint8
+FP8X4 = mybir.dt.float8_e4m3fn_x4
+ALU = mybir.AluOpType
+ACT = mybir.ActivationFunctionType
+
+P = 128
+R = 4096
+DI = 1024
+DO = 1024
+RB = 512
+NB = R // RB
+NJ = DO // P
+LN_EPS = 1e-5
+FLOPS = 2 * R * DI * DO
+
+MANUAL = True
+
+
+def tile_onebitlinear_t_kernel(
+    tc, x, weight, in_channel_scale, out_channel_scale, bias, ln_gamma, ln_beta, out
+):
+    nc = tc.nc
+    x_blk = x.flatten_outer_dims().rearrange("(i p c) k -> i p c k", p=P, c=4)
+    o_blk = out.flatten_outer_dims().rearrange("(i p c) n -> i c p n", p=P, c=4)
+    w_v = weight.rearrange("(j p) k -> p j k", p=P)
+
+    with ExitStack() as ctx:
+        const = ctx.enter_context(tc.tile_pool(name="const", bufs=1))
+        xpool = ctx.enter_context(tc.tile_pool(name="xpool", bufs=3))
+        qpool = ctx.enter_context(tc.tile_pool(name="qpool", bufs=2))
+        hpool = ctx.enter_context(tc.tile_pool(name="hpool", bufs=2))
+        ypool = ctx.enter_context(tc.tile_pool(name="ypool", bufs=5))
+        small = ctx.enter_context(tc.tile_pool(name="small", bufs=6))
+        psum = ctx.enter_context(tc.psum_pool(name="psum", bufs=2))
+        if MANUAL:
+            ctx.enter_context(tc.manual_schedule())
+
+        x_sb = {}
+        xg = {}
+        xq = {}
+        xsc = {}
+        xt = {}
+        hT = {}
+        ht = {}
+        yt = {}
+        mvs = {}
+        sds = {}
+        rstds = {}
+
+        def load_x(b):
+            xs = xpool.tile([P, 4, DI], BF16, name="xs")
+            nc.sync.dma_start(out=xs[:], in_=x_blk[b])
+            x_sb[b] = xs
+
+        load_x(0)
+        w_sb = const.tile([P, NJ, DI], BF16, name="w_sb")
+        for q in range(4):
+            nc.sync.dma_start(out=w_sb[:, 2 * q : 2 * q + 2, :], in_=w_v[:, 2 * q : 2 * q + 2, :])
+        load_x(1)
+        load_x(2)
+
+        ident = const.tile([P, P], F32, name="ident")
+        make_identity(nc, ident[:])
+        ics_t = const.tile([P, 8], BF16, name="ics_t")
+        s16 = const.tile([P, NJ], BF16, name="s16")
+        b16 = const.tile([P, NJ], BF16, name="b16")
+        with nc.allow_non_contiguous_dma(reason="small per-partition vectors"):
+            nc.scalar.dma_start(
+                out=ics_t[:].rearrange("p (a e) -> p a e", e=2),
+                in_=in_channel_scale.rearrange("(a p e) -> p a e", a=4, e=2),
+            )
+            nc.scalar.dma_start(out=s16[:], in_=out_channel_scale.rearrange("(j p) -> p j", p=P))
+            nc.scalar.dma_start(out=b16[:], in_=bias.rearrange("(j p) -> p j", p=P))
+        g16 = const.tile([P, DO], BF16, name="g16")
+        be16 = const.tile([P, DO], BF16, name="be16")
+        nc.gpsimd.dma_start(out=g16[:], in_=ln_gamma.partition_broadcast(P))
+        nc.gpsimd.dma_start(out=be16[:], in_=ln_beta.partition_broadcast(P))
+        s_t = const.tile([P, NJ], F32, name="s_t")
+        b_t = const.tile([P, NJ], F32, name="b_t")
+        nc.vector.tensor_copy(out=s_t[:], in_=s16[:])
+        nc.vector.tensor_copy(out=b_t[:], in_=b16[:])
+        g_b = const.tile([P, DO], F32, name="g_b")
+        be_b = const.tile([P, DO], F32, name="be_b")
+        eps_t = const.tile([P, 1], F32, name="eps_t")
+        nc.vector.memset(eps_t[:], LN_EPS)
+        sgn_b = const.tile([P, 1], F32, name="sgn_b")
+        nc.vector.memset(sgn_b[:], 2.0 ** -80)
+
+        wg = const.tile([P, 2, DO, 4], BF16, name="wg", align_bytes=64)
+        wq = const.tile([P, 2, DO], U32, name="wq", align_bytes=64)
+        wsc = const.tile([P, 2, DO], U8, name="wsc", align_bytes=64)
+
+        def w_tile(j):
+            wt = psum.tile([P, 512], F32, name="wt", tag="xt")
+            wj = w_sb[:, j, :].bitcast(F32)
+            for a in range(4):
+                nc.tensor.transpose(wt[:, a * P : (a + 1) * P], wj[:, a * P : (a + 1) * P], ident[:])
+            wv = wt[:].bitcast(BF16)
+            nc.scalar.activation(
+                out=wg[:, 0, j * P : (j + 1) * P, :].rearrange("p n (u e) -> p n u e", u=2),
+                in_=wv[:, 0:512].rearrange("p (u n e) -> p n u e", u=2, e=2),
+                func=ACT.Sign,
+                bias=sgn_b[:, 0:1],
+                scale=2.0 ** 64,
+            )
+            nc.vector.tensor_scalar(
+                out=wg[:, 1, j * P : (j + 1) * P, :].rearrange("p n (u e) -> p n u e", u=2),
+                in0=wv[:, 512:1024].rearrange("p (u n e) -> p n u e", u=2, e=2),
+                scalar1=0.0,
+                scalar2=2.0,
+                op0=ALU.is_ge,
+                op1=ALU.mult,
+            )
+
+        def w_quant(q):
+            cols = slice(256 * q, 256 * (q + 1))
+            half = wg[:, 1, cols, :].rearrange("p n t -> p (n t)")
+            nc.vector.tensor_scalar_add(out=half, in0=half, scalar1=-1.0)
+            for g in range(2):
+                nc.vector.quantize_mx(
+                    out=wq[:, g, cols].bitcast(FP8X4),
+                    scales=wsc[:, g, cols],
+                    in_=wg[:, g, cols, :].rearrange("p n t -> p (n t)"),
+                )
+
+        def a_pe(b, qa):
+            g, hh = divmod(qa, 2)
+            t = psum.tile([P, 512], F32, name="xtb", tag="xt")
+            for u in range(2):
+                for cc in range(2):
+                    k0 = (2 * g + u) * P
+                    nc.tensor.transpose(
+                        t[:, (2 * u + cc) * P : (2 * u + cc + 1) * P],
+                        x_sb[b][:, 2 * hh + cc, :].bitcast(F32)[:, k0 : k0 + P],
+                        ident[:],
+                    )
+            xt[(b, qa)] = t
+
+        def a_v(b, qa):
+            g, hh = divmod(qa, 2)
+            if qa == 0:
+                xgt = qpool.tile([P, 2, RB, 4], BF16, name="xgt", align_bytes=64)
+                xg[b] = xgt
+            nc.vector.tensor_tensor(
+                out=xg[b][:, g, hh * 256 : (hh + 1) * 256, :].rearrange("p m (u e) -> p m u e", u=2),
+                in0=xt[(b, qa)][:].bitcast(BF16).rearrange("p (u m e) -> p m u e", u=2, e=2),
+                in1=ics_t[:, 4 * g : 4 * g + 4]
+                .rearrange("p (u e) -> p u e", u=2)
+                .unsqueeze(1)
+                .to_broadcast([P, 256, 2, 2]),
+                op=ALU.mult,
+            )
+
+        def a_quant(b, g):
+            if g == 0:
+                xqt = qpool.tile([P, 2, RB], U32, name="xqt", align_bytes=64)
+                xst = qpool.tile([P, 2, RB], U8, name="xst", align_bytes=64)
+                xq[b] = xqt
+                xsc[b] = xst
+            nc.vector.quantize_mx(
+                out=xq[b][:, g, :].bitcast(FP8X4),
+                scales=xsc[b][:, g, :],
+                in_=xg[b][:, g, :, :].rearrange("p m t -> p (m t)"),
+            )
+
+        def m_tile(b, j):
+            if j == 0:
+                hTt = hpool.tile([P, NJ, RB], F32, name="hTt")
+                hT[b] = hTt
+            acc = psum.tile([P, RB], F32, name="acc", tag="acc")
+            for g in range(2):
+                nc.tensor.matmul_mx(
+                    out=acc[:],
+                    lhsT=wq[:, g, j * P : (j + 1) * P].bitcast(FP8X4),
+                    lhsT_scale=wsc[:, g, j * P : (j + 1) * P],
+                    rhs=xq[b][:, g, :].bitcast(FP8X4),
+                    rhs_scale=xsc[b][:, g, :],
+                    start=(g == 0),
+                    stop=(g == 1),
+                )
+            nc.scalar.activation(
+                out=hT[b][:, j, :],
+                in_=acc[:],
+                func=ACT.Identity,
+                bias=b_t[:, j : j + 1],
+                scale=s_t[:, j : j + 1],
+            )
+
+        def h_pe(b, c):
+            for hn in range(2):
+                t = psum.tile([P, 512], F32, name="htb", tag="ht", bufs=4)
+                for jj in range(4):
+                    nc.tensor.transpose(
+                        t[:, jj * P : (jj + 1) * P],
+                        hT[b][:, 4 * hn + jj, c * P : (c + 1) * P],
+                        ident[:],
+                    )
+                ht[(b, c, hn)] = t
+
+        def h_v(b, c):
+            st = small.tile([P, 2, 6], F32, name="st")
+            for hn in range(2):
+                nc.vector.bn_stats(out=st[:, hn, :], in_=ht[(b, c, hn)][:])
+            mv = small.tile([P, 2], F32, name="mv")
+            nc.vector.bn_aggr(out=mv[:], in_=st[:].rearrange("p h s -> p (h s)"))
+            mvs[(b, c)] = mv
+            y = ypool.tile([P, DO], F32, name="y")
+            yt[(b, c)] = y
+            for hn in range(2):
+                nc.vector.scalar_tensor_tensor(
+                    out=y[:, hn * 512 : (hn + 1) * 512],
+                    in0=ht[(b, c, hn)][:],
+                    scalar=mv[:, 0:1],
+                    in1=g_b[:, hn * 512 : (hn + 1) * 512],
+                    op0=ALU.subtract,
+                    op1=ALU.mult,
+                )
+
+        def h_sqrt(b, c):
+            sd = small.tile([P, 1], F32, name="sd")
+            nc.scalar.activation(
+                out=sd[:], in_=mvs[(b, c)][:, 1:2], func=ACT.Sqrt, bias=eps_t[:, 0:1], scale=1.0
+            )
+            sds[(b, c)] = sd
+
+        def h_recip(b, c):
+            rs = small.tile([P, 1], F32, name="rs")
+            nc.vector.reciprocal(out=rs[:], in_=sds[(b, c)][:])
+            rstds[(b, c)] = rs
+
+        def h_s(b, c):
+            y = yt[(b, c)]
+            nc.scalar.activation(out=y[:], in_=y[:], func=ACT.Copy, scale=rstds[(b, c)][:, 0:1])
+
+        def h_g(b, c):
+            y = yt[(b, c)]
+            nc.gpsimd.tensor_tensor(out=y[:], in0=y[:], in1=be_b[:], op=ALU.add)
+            nc.sync.dma_start(out=o_blk[b, c], in_=y[:])
+
+        def at(t, off):
+            b, q = divmod(t - off, 4)
+            if 0 <= b < NB:
+                return b, q
+            return None
+
+        for t in range(-6, 4 * NB + 8):
+            if -4 <= t < 0:
+                w_tile(2 * (t + 4))
+                w_tile(2 * (t + 4) + 1)
+            e = at(t, 6)
+            if e:
+                h_recip(e[0], e[1])
+            e = at(t, 0)
+            if e:
+                m_tile(e[0], 2 * e[1])
+                m_tile(e[0], 2 * e[1] + 1)
+            e = at(t, 4)
+            if e:
+                h_pe(e[0], e[1])
+            e = at(t, -6)
+            if e:
+                a_pe(e[0], e[1])
+            e = at(t, 5)
+            if e:
+                h_v(e[0], e[1])
+            e = at(t, -5)
+            if e:
+                a_v(e[0], e[1])
+            e = at(t, 6)
+            if e:
+                h_s(e[0], e[1])
+            e = at(t, 5)
+            if e:
+                h_sqrt(e[0], e[1])
+            e = at(t, 7)
+            if e:
+                h_g(e[0], e[1])
+            if -3 <= t < 1:
+                w_quant(t + 3)
+            if t == 2:
+                nc.vector.tensor_copy(out=g_b[:], in_=g16[:])
+                nc.vector.tensor_copy(out=be_b[:], in_=be16[:])
+            e = at(t, -3)
+            if e and e[1] == 0:
+                a_quant(e[0], 0)
+            e = at(t, -1)
+            if e and e[1] == 0:
+                a_quant(e[0], 1)
+            e = at(t, -14)
+            if e and e[1] == 0 and e[0] >= 3:
+                load_x(e[0])

@@ -22,19 +22,27 @@ LN_EPS = 1e-5
 FLOPS = 2 * R * DI * DO
 
 MANUAL = True
+XS_BUFS = 3
+
+
+def post_kind(b, c):
+    if b == NB - 1 and c == 3:
+        return "V"
+    return "SG"
 
 
 def tile_onebitlinear_t_kernel(
     tc, x, weight, in_channel_scale, out_channel_scale, bias, ln_gamma, ln_beta, out
 ):
     nc = tc.nc
-    x_blk = x.flatten_outer_dims().rearrange("(i p c) k -> i p c k", p=P, c=4)
-    o_blk = out.flatten_outer_dims().rearrange("(i p c) n -> i c p n", p=P, c=4)
-    w_v = weight.rearrange("(j p) k -> p j k", p=P)
+    x_blk = x.rearrange("b s (q k) -> (b s q) k", q=4).rearrange("(i t p) k -> i p t k", t=16, p=P)
+    w_v = weight.rearrange("n (q k) -> (n q) k", q=4).rearrange("(j t p) k -> p j t k", t=4, p=P)
+    o_blk = out.flatten_outer_dims().rearrange("(i c p) n -> i c p n", p=P, c=4)
 
     with ExitStack() as ctx:
         const = ctx.enter_context(tc.tile_pool(name="const", bufs=1))
-        xpool = ctx.enter_context(tc.tile_pool(name="xpool", bufs=3))
+        xpool = ctx.enter_context(tc.tile_pool(name="xpool", bufs=XS_BUFS))
+        gpool = ctx.enter_context(tc.tile_pool(name="gpool", bufs=2))
         qpool = ctx.enter_context(tc.tile_pool(name="qpool", bufs=2))
         hpool = ctx.enter_context(tc.tile_pool(name="hpool", bufs=2))
         ypool = ctx.enter_context(tc.tile_pool(name="ypool", bufs=5))
@@ -52,20 +60,12 @@ def tile_onebitlinear_t_kernel(
         ht = {}
         yt = {}
         mvs = {}
-        sds = {}
         rstds = {}
 
         def load_x(b):
-            xs = xpool.tile([P, 4, DI], BF16, name="xs")
+            xs = xpool.tile([P, 16, 256], BF16, name="xs")
             nc.sync.dma_start(out=xs[:], in_=x_blk[b])
             x_sb[b] = xs
-
-        load_x(0)
-        w_sb = const.tile([P, NJ, DI], BF16, name="w_sb")
-        for q in range(4):
-            nc.sync.dma_start(out=w_sb[:, 2 * q : 2 * q + 2, :], in_=w_v[:, 2 * q : 2 * q + 2, :])
-        load_x(1)
-        load_x(2)
 
         ident = const.tile([P, P], F32, name="ident")
         make_identity(nc, ident[:])
@@ -83,12 +83,22 @@ def tile_onebitlinear_t_kernel(
         be16 = const.tile([P, DO], BF16, name="be16")
         nc.gpsimd.dma_start(out=g16[:], in_=ln_gamma.partition_broadcast(P))
         nc.gpsimd.dma_start(out=be16[:], in_=ln_beta.partition_broadcast(P))
+
+        w_sb = const.tile([P, NJ, 4, 256], BF16, name="w_sb")
+
+        def load_w(q):
+            nc.sync.dma_start(out=w_sb[:, 2 * q : 2 * q + 2], in_=w_v[:, 2 * q : 2 * q + 2])
+
+        load_x(0)
+        load_w(0)
+        load_w(1)
+        load_x(1)
+        load_w(2)
+        load_w(3)
+        load_x(2)
+
         s_t = const.tile([P, NJ], F32, name="s_t")
         b_t = const.tile([P, NJ], F32, name="b_t")
-        nc.vector.tensor_copy(out=s_t[:], in_=s16[:])
-        nc.vector.tensor_copy(out=b_t[:], in_=b16[:])
-        g_b = const.tile([P, DO], F32, name="g_b")
-        be_b = const.tile([P, DO], F32, name="be_b")
         eps_t = const.tile([P, 1], F32, name="eps_t")
         nc.vector.memset(eps_t[:], LN_EPS)
         sgn_b = const.tile([P, 1], F32, name="sgn_b")
@@ -98,32 +108,27 @@ def tile_onebitlinear_t_kernel(
         wq = const.tile([P, 2, DO], U32, name="wq", align_bytes=64)
         wsc = const.tile([P, 2, DO], U8, name="wsc", align_bytes=64)
 
-        def w_tile(j):
-            wt = psum.tile([P, 512], F32, name="wt", tag="xt")
-            wj = w_sb[:, j, :].bitcast(F32)
+        def w_pe(j):
+            wt = psum.tile([P, 512], F32, name="wt", tag="ht", bufs=4)
             for a in range(4):
-                nc.tensor.transpose(wt[:, a * P : (a + 1) * P], wj[:, a * P : (a + 1) * P], ident[:])
-            wv = wt[:].bitcast(BF16)
-            nc.scalar.activation(
-                out=wg[:, 0, j * P : (j + 1) * P, :].rearrange("p n (u e) -> p n u e", u=2),
-                in_=wv[:, 0:512].rearrange("p (u n e) -> p n u e", u=2, e=2),
-                func=ACT.Sign,
-                bias=sgn_b[:, 0:1],
-                scale=2.0 ** 64,
-            )
-            nc.vector.tensor_scalar(
-                out=wg[:, 1, j * P : (j + 1) * P, :].rearrange("p n (u e) -> p n u e", u=2),
-                in0=wv[:, 512:1024].rearrange("p (u n e) -> p n u e", u=2, e=2),
-                scalar1=0.0,
-                scalar2=2.0,
-                op0=ALU.is_ge,
-                op1=ALU.mult,
-            )
+                nc.tensor.transpose(wt[:, a * P : (a + 1) * P], w_sb[:, j, a, :].bitcast(F32), ident[:])
+            xt[("w", j)] = wt
+
+        def w_sign(j):
+            src = xt[("w", j)][:].bitcast(BF16).rearrange("p (n g t) -> p n g t", g=2, t=4)
+            dst = wg[:, :, j * P : (j + 1) * P, :].rearrange("p g n t -> p n g t")
+            if j % 2 == 0:
+                nc.scalar.activation(out=dst, in_=src, func=ACT.Sign, bias=sgn_b[:, 0:1], scale=2.0 ** 64)
+            else:
+                nc.vector.tensor_scalar(
+                    out=dst, in0=src, scalar1=0.0, scalar2=2.0, op0=ALU.is_ge, op1=ALU.mult
+                )
 
         def w_quant(q):
+            j = 2 * q + 1
+            odd = wg[:, :, j * P : (j + 1) * P, :].rearrange("p g n t -> p g (n t)")
+            nc.vector.tensor_scalar_add(out=odd, in0=odd, scalar1=-1.0)
             cols = slice(256 * q, 256 * (q + 1))
-            half = wg[:, 1, cols, :].rearrange("p n t -> p (n t)")
-            nc.vector.tensor_scalar_add(out=half, in0=half, scalar1=-1.0)
             for g in range(2):
                 nc.vector.quantize_mx(
                     out=wq[:, g, cols].bitcast(FP8X4),
@@ -132,44 +137,37 @@ def tile_onebitlinear_t_kernel(
                 )
 
         def a_pe(b, qa):
-            g, hh = divmod(qa, 2)
             t = psum.tile([P, 512], F32, name="xtb", tag="xt")
-            for u in range(2):
-                for cc in range(2):
-                    k0 = (2 * g + u) * P
-                    nc.tensor.transpose(
-                        t[:, (2 * u + cc) * P : (2 * u + cc + 1) * P],
-                        x_sb[b][:, 2 * hh + cc, :].bitcast(F32)[:, k0 : k0 + P],
-                        ident[:],
-                    )
+            for a in range(4):
+                nc.tensor.transpose(
+                    t[:, a * P : (a + 1) * P], x_sb[b][:, 4 * qa + a, :].bitcast(F32), ident[:]
+                )
             xt[(b, qa)] = t
 
         def a_v(b, qa):
-            g, hh = divmod(qa, 2)
             if qa == 0:
-                xgt = qpool.tile([P, 2, RB, 4], BF16, name="xgt", align_bytes=64)
+                xgt = gpool.tile([P, 2, RB, 4], BF16, name="xgt", align_bytes=64)
                 xg[b] = xgt
             nc.vector.tensor_tensor(
-                out=xg[b][:, g, hh * 256 : (hh + 1) * 256, :].rearrange("p m (u e) -> p m u e", u=2),
-                in0=xt[(b, qa)][:].bitcast(BF16).rearrange("p (u m e) -> p m u e", u=2, e=2),
-                in1=ics_t[:, 4 * g : 4 * g + 4]
-                .rearrange("p (u e) -> p u e", u=2)
-                .unsqueeze(1)
-                .to_broadcast([P, 256, 2, 2]),
+                out=xg[b][:, :, qa * P : (qa + 1) * P, :].rearrange("p g m t -> p m g t"),
+                in0=xt[(b, qa)][:].bitcast(BF16).rearrange("p (m g t) -> p m g t", g=2, t=4),
+                in1=ics_t[:].rearrange("p (g t) -> p g t", g=2).unsqueeze(1).to_broadcast([P, P, 2, 4]),
                 op=ALU.mult,
             )
 
-        def a_quant(b, g):
-            if g == 0:
+        def a_quant(b, h):
+            if h == 0:
                 xqt = qpool.tile([P, 2, RB], U32, name="xqt", align_bytes=64)
                 xst = qpool.tile([P, 2, RB], U8, name="xst", align_bytes=64)
                 xq[b] = xqt
                 xsc[b] = xst
-            nc.vector.quantize_mx(
-                out=xq[b][:, g, :].bitcast(FP8X4),
-                scales=xsc[b][:, g, :],
-                in_=xg[b][:, g, :, :].rearrange("p m t -> p (m t)"),
-            )
+            cols = slice(256 * h, 256 * (h + 1))
+            for g in range(2):
+                nc.vector.quantize_mx(
+                    out=xq[b][:, g, cols].bitcast(FP8X4),
+                    scales=xsc[b][:, g, cols],
+                    in_=xg[b][:, g, cols, :].rearrange("p m t -> p (m t)"),
+                )
 
         def m_tile(b, j):
             if j == 0:
@@ -205,44 +203,60 @@ def tile_onebitlinear_t_kernel(
                     )
                 ht[(b, c, hn)] = t
 
-        def h_v(b, c):
+        def h_st(b, c):
             st = small.tile([P, 2, 6], F32, name="st")
             for hn in range(2):
                 nc.vector.bn_stats(out=st[:, hn, :], in_=ht[(b, c, hn)][:])
             mv = small.tile([P, 2], F32, name="mv")
             nc.vector.bn_aggr(out=mv[:], in_=st[:].rearrange("p h s -> p (h s)"))
             mvs[(b, c)] = mv
+
+        def h_b(b, c):
             y = ypool.tile([P, DO], F32, name="y")
             yt[(b, c)] = y
             for hn in range(2):
                 nc.vector.scalar_tensor_tensor(
                     out=y[:, hn * 512 : (hn + 1) * 512],
                     in0=ht[(b, c, hn)][:],
-                    scalar=mv[:, 0:1],
-                    in1=g_b[:, hn * 512 : (hn + 1) * 512],
+                    scalar=mvs[(b, c)][:, 0:1],
+                    in1=g16[:, hn * 512 : (hn + 1) * 512],
                     op0=ALU.subtract,
                     op1=ALU.mult,
                 )
 
-        def h_sqrt(b, c):
-            sd = small.tile([P, 1], F32, name="sd")
-            nc.scalar.activation(
-                out=sd[:], in_=mvs[(b, c)][:, 1:2], func=ACT.Sqrt, bias=eps_t[:, 0:1], scale=1.0
-            )
-            sds[(b, c)] = sd
-
-        def h_recip(b, c):
+        def h_rs(b, c):
             rs = small.tile([P, 1], F32, name="rs")
-            nc.vector.reciprocal(out=rs[:], in_=sds[(b, c)][:])
+            nc.scalar.activation(
+                out=rs[:],
+                in_=mvs[(b, c)][:, 1:2],
+                func=ACT.Abs_reciprocal_sqrt,
+                bias=eps_t[:, 0:1],
+                scale=1.0,
+            )
             rstds[(b, c)] = rs
 
         def h_s(b, c):
             y = yt[(b, c)]
-            nc.scalar.activation(out=y[:], in_=y[:], func=ACT.Copy, scale=rstds[(b, c)][:, 0:1])
+            if post_kind(b, c) == "V":
+                for hn in range(2):
+                    cols = slice(hn * 512, (hn + 1) * 512)
+                    nc.vector.scalar_tensor_tensor(
+                        out=y[:, cols],
+                        in0=y[:, cols],
+                        scalar=rstds[(b, c)][:, 0:1],
+                        in1=be16[:, cols],
+                        op0=ALU.mult,
+                        op1=ALU.add,
+                    )
+                    nc.sync.dma_start(out=o_blk[b, c][:, cols], in_=y[:, cols])
+            else:
+                nc.scalar.activation(out=y[:], in_=y[:], func=ACT.Copy, scale=rstds[(b, c)][:, 0:1])
 
         def h_g(b, c):
+            if post_kind(b, c) == "V":
+                return
             y = yt[(b, c)]
-            nc.gpsimd.tensor_tensor(out=y[:], in0=y[:], in1=be_b[:], op=ALU.add)
+            nc.gpsimd.tensor_tensor(out=y[:], in0=y[:], in1=be16[:], op=ALU.add)
             nc.sync.dma_start(out=o_blk[b, c], in_=y[:])
 
         def at(t, off):
@@ -251,13 +265,17 @@ def tile_onebitlinear_t_kernel(
                 return b, q
             return None
 
-        for t in range(-6, 4 * NB + 8):
-            if -4 <= t < 0:
-                w_tile(2 * (t + 4))
-                w_tile(2 * (t + 4) + 1)
-            e = at(t, 6)
+        for t in range(-6, 4 * NB + 11):
+            e = at(t, -5)
             if e:
-                h_recip(e[0], e[1])
+                a_v(e[0], e[1])
+            e = at(t, -6)
+            if e:
+                a_pe(e[0], e[1])
+            if -4 <= t < 0:
+                for j in (2 * (t + 4), 2 * (t + 4) + 1):
+                    w_pe(j)
+                    w_sign(j)
             e = at(t, 0)
             if e:
                 m_tile(e[0], 2 * e[1])
@@ -265,35 +283,28 @@ def tile_onebitlinear_t_kernel(
             e = at(t, 4)
             if e:
                 h_pe(e[0], e[1])
-            e = at(t, -6)
-            if e:
-                a_pe(e[0], e[1])
             e = at(t, 5)
             if e:
-                h_v(e[0], e[1])
-            e = at(t, -5)
-            if e:
-                a_v(e[0], e[1])
+                h_st(e[0], e[1])
+                h_rs(e[0], e[1])
+                h_b(e[0], e[1])
             e = at(t, 6)
             if e:
                 h_s(e[0], e[1])
-            e = at(t, 5)
-            if e:
-                h_sqrt(e[0], e[1])
             e = at(t, 7)
             if e:
                 h_g(e[0], e[1])
             if -3 <= t < 1:
                 w_quant(t + 3)
-            if t == 2:
-                nc.vector.tensor_copy(out=g_b[:], in_=g16[:])
-                nc.vector.tensor_copy(out=be_b[:], in_=be16[:])
+            if t == -1:
+                nc.vector.tensor_copy(out=s_t[:], in_=s16[:])
+                nc.vector.tensor_copy(out=b_t[:], in_=b16[:])
             e = at(t, -3)
             if e and e[1] == 0:
                 a_quant(e[0], 0)
             e = at(t, -1)
             if e and e[1] == 0:
                 a_quant(e[0], 1)
-            e = at(t, -14)
-            if e and e[1] == 0 and e[0] >= 3:
+            e = at(t, -13)
+            if e and e[1] == 0 and e[0] >= XS_BUFS:
                 load_x(e[0])

@@ -21,7 +21,7 @@ NJ = DO // P
 LN_EPS = 1e-5
 FLOPS = 2 * R * DI * DO
 
-MANUAL = True
+MANUAL = False
 XS_BUFS = 3
 
 

@@ -64,7 +64,10 @@ def tile_onebitlinear_t_kernel(
 
         def load_x(b):
             xs = xpool.tile([P, 16, 256], BF16, name="xs")
-            nc.sync.dma_start(out=xs[:], in_=x_blk[b])
+            parts = 4 if b == 0 else 1
+            for i in range(parts):
+                ts = slice(i * 16 // parts, (i + 1) * 16 // parts)
+                nc.sync.dma_start(out=xs[:, ts, :], in_=x_blk[b][:, ts, :])
             x_sb[b] = xs
 
         ident = const.tile([P, P], F32, name="ident")
@@ -155,19 +158,16 @@ def tile_onebitlinear_t_kernel(
                 op=ALU.mult,
             )
 
-        def a_quant(b, h):
-            if h == 0:
-                xqt = qpool.tile([P, 2, RB], U32, name="xqt", align_bytes=64)
-                xst = qpool.tile([P, 2, RB], U8, name="xst", align_bytes=64)
-                xq[b] = xqt
-                xsc[b] = xst
-            cols = slice(256 * h, 256 * (h + 1))
-            for g in range(2):
-                nc.vector.quantize_mx(
-                    out=xq[b][:, g, cols].bitcast(FP8X4),
-                    scales=xsc[b][:, g, cols],
-                    in_=xg[b][:, g, cols, :].rearrange("p m t -> p (m t)"),
-                )
+        def a_quant(b):
+            xqt = qpool.tile([P, 2, RB], U32, name="xqt", align_bytes=64)
+            xst = qpool.tile([P, 2, RB], U8, name="xst", align_bytes=64)
+            xq[b] = xqt
+            xsc[b] = xst
+            nc.vector.quantize_mx(
+                out=xqt[:].rearrange("p g m -> p (g m)").bitcast(FP8X4),
+                scales=xst[:].rearrange("p g m -> p (g m)"),
+                in_=xg[b][:].rearrange("p g m t -> p (g m t)"),
+            )
 
         def m_tile(b, j):
             if j == 0:
@@ -299,12 +299,9 @@ def tile_onebitlinear_t_kernel(
             if t == -1:
                 nc.vector.tensor_copy(out=s_t[:], in_=s16[:])
                 nc.vector.tensor_copy(out=b_t[:], in_=b16[:])
-            e = at(t, -3)
-            if e and e[1] == 0:
-                a_quant(e[0], 0)
             e = at(t, -1)
             if e and e[1] == 0:
-                a_quant(e[0], 1)
+                a_quant(e[0])
             e = at(t, -13)
             if e and e[1] == 0 and e[0] >= XS_BUFS:
                 load_x(e[0])

@@ -72,20 +72,46 @@ def tile_onebitlinear_t_kernel(
 
         ident = const.tile([P, P], F32, name="ident")
         make_identity(nc, ident[:])
-        ics_t = const.tile([P, 8], BF16, name="ics_t")
-        s16 = const.tile([P, NJ], BF16, name="s16")
-        b16 = const.tile([P, NJ], BF16, name="b16")
-        with nc.allow_non_contiguous_dma(reason="small per-partition vectors"):
-            nc.scalar.dma_start(
-                out=ics_t[:].rearrange("p (a e) -> p a e", e=2),
-                in_=in_channel_scale.rearrange("(a p e) -> p a e", a=4, e=2),
-            )
-            nc.scalar.dma_start(out=s16[:], in_=out_channel_scale.rearrange("(j p) -> p j", p=P))
-            nc.scalar.dma_start(out=b16[:], in_=bias.rearrange("(j p) -> p j", p=P))
+        vrow = const.tile([P, P], F32, name="vrow")
+        nc.vector.memset(vrow[:], 0.0)
+        sb16 = const.tile([P, P], BF16, name="sb16")
+        nc.vector.memset(sb16[:], 0.0)
+        gz = const.tile([P, 2, DO], BF16, name="gz")
+        nc.vector.memset(gz[:], 0.0)
+        ones = const.tile([P, P], BF16, name="ones")
+        nc.vector.memset(ones[:], 1.0)
+        nc.scalar.dma_start(
+            out=vrow[0:4, :].bitcast(BF16), in_=in_channel_scale.rearrange("(a k) -> a k", a=4)
+        )
+        nc.scalar.dma_start(out=sb16[0:8, :], in_=out_channel_scale.rearrange("(j p) -> j p", p=P))
+        nc.scalar.dma_start(out=sb16[8:16, :], in_=bias.rearrange("(j p) -> j p", p=P))
+        nc.scalar.dma_start(out=gz[0:1, 0, :], in_=ln_gamma.rearrange("(o n) -> o n", o=1))
+        nc.scalar.dma_start(out=gz[0:1, 1, :], in_=ln_beta.rearrange("(o n) -> o n", o=1))
+        ics_w = const.tile([P, 4], F32, name="ics_w")
+        ics_t = ics_w[:].bitcast(BF16)
+        sbf = const.tile([P, P], F32, name="sbf")
+        sb_t = const.tile([P, 16], F32, name="sb_t")
         g16 = const.tile([P, DO], BF16, name="g16")
         be16 = const.tile([P, DO], BF16, name="be16")
-        nc.gpsimd.dma_start(out=g16[:], in_=ln_gamma.partition_broadcast(P))
-        nc.gpsimd.dma_start(out=be16[:], in_=ln_beta.partition_broadcast(P))
+
+        def spread_ics():
+            pt = psum.tile([P, 512], F32, name="pt", tag="ht", bufs=4)
+            nc.tensor.transpose(pt[:, 0:P], vrow[:], ident[:])
+            nc.vector.tensor_copy(out=ics_w[:], in_=pt[:, 0:4])
+
+        def spread_sb():
+            nc.vector.tensor_copy(out=sbf[:], in_=sb16[:])
+            pt = psum.tile([P, 512], F32, name="pt", tag="ht", bufs=4)
+            nc.tensor.transpose(pt[:, 0:P], sbf[:], ident[:])
+            nc.vector.tensor_copy(out=sb_t[:], in_=pt[:, 0:16])
+
+        def spread_gb():
+            for v, dst in ((0, g16), (1, be16)):
+                for hn in range(2):
+                    cols = slice(hn * 512, (hn + 1) * 512)
+                    pt = psum.tile([P, 512], F32, name="pt", tag="ht", bufs=4)
+                    nc.tensor.matmul(pt[:], lhsT=ones[:], rhs=gz[:, v, cols], start=True, stop=True)
+                    nc.scalar.copy(out=dst[:, cols], in_=pt[:])
 
         w_sb = const.tile([P, NJ, 4, 256], BF16, name="w_sb")
 
@@ -100,8 +126,8 @@ def tile_onebitlinear_t_kernel(
         load_w(3)
         load_x(2)
 
-        s_t = const.tile([P, NJ], F32, name="s_t")
-        b_t = const.tile([P, NJ], F32, name="b_t")
+        s_t = sb_t[:, 0:NJ]
+        b_t = sb_t[:, NJ : 2 * NJ]
         eps_t = const.tile([P, 1], F32, name="eps_t")
         nc.vector.memset(eps_t[:], LN_EPS)
         sgn_b = const.tile([P, 1], F32, name="sgn_b")
@@ -154,7 +180,7 @@ def tile_onebitlinear_t_kernel(
             nc.vector.tensor_tensor(
                 out=xg[b][:, :, qa * P : (qa + 1) * P, :].rearrange("p g m t -> p m g t"),
                 in0=xt[(b, qa)][:].bitcast(BF16).rearrange("p (m g t) -> p m g t", g=2, t=4),
-                in1=ics_t[:].rearrange("p (g t) -> p g t", g=2).unsqueeze(1).to_broadcast([P, P, 2, 4]),
+                in1=ics_t.rearrange("p (g t) -> p g t", g=2).unsqueeze(1).to_broadcast([P, P, 2, 4]),
                 op=ALU.mult,
             )
 
@@ -265,6 +291,7 @@ def tile_onebitlinear_t_kernel(
                 return b, q
             return None
 
+        spread_ics()
         for t in range(-6, 4 * NB + 11):
             e = at(t, -5)
             if e:
@@ -297,8 +324,8 @@ def tile_onebitlinear_t_kernel(
             if -3 <= t < 1:
                 w_quant(t + 3)
             if t == -1:
-                nc.vector.tensor_copy(out=s_t[:], in_=s16[:])
-                nc.vector.tensor_copy(out=b_t[:], in_=b16[:])
+                spread_sb()
+                spread_gb()
             e = at(t, -1)
             if e and e[1] == 0:
                 a_quant(e[0])

@@ -35,9 +35,9 @@ def tile_onebitlinear_t_kernel(
     tc, x, weight, in_channel_scale, out_channel_scale, bias, ln_gamma, ln_beta, out
 ):
     nc = tc.nc
-    x_blk = x.rearrange("b s (q k) -> (b s q) k", q=4).rearrange("(i t p) k -> i p t k", t=16, p=P)
-    w_v = weight.rearrange("n (q k) -> (n q) k", q=4).rearrange("(j t p) k -> p j t k", t=4, p=P)
-    o_blk = out.flatten_outer_dims().rearrange("(i c p) n -> i c p n", p=P, c=4)
+    x_blk = x.flatten_outer_dims().rearrange("(i p c) k -> i p c k", p=P, c=4)
+    w_v = weight.rearrange("(j p) k -> p j k", p=P)
+    o_blk = out.flatten_outer_dims().rearrange("(i p c) n -> i c p n", p=P, c=4)
 
     with ExitStack() as ctx:
         const = ctx.enter_context(tc.tile_pool(name="const", bufs=1))
@@ -63,10 +63,10 @@ def tile_onebitlinear_t_kernel(
         rstds = {}
 
         def load_x(b):
-            xs = xpool.tile([P, 16, 256], BF16, name="xs")
-            parts = 4 if b == 0 else 1
+            xs = xpool.tile([P, 4, DI], BF16, name="xs")
+            parts = 2 if b == 0 else 1
             for i in range(parts):
-                ts = slice(i * 16 // parts, (i + 1) * 16 // parts)
+                ts = slice(i * 4 // parts, (i + 1) * 4 // parts)
                 nc.sync.dma_start(out=xs[:, ts, :], in_=x_blk[b][:, ts, :])
             x_sb[b] = xs
 
@@ -113,7 +113,7 @@ def tile_onebitlinear_t_kernel(
                     nc.tensor.matmul(pt[:], lhsT=ones[:], rhs=gz[:, v, cols], start=True, stop=True)
                     nc.scalar.copy(out=dst[:, cols], in_=pt[:])
 
-        w_sb = const.tile([P, NJ, 4, 256], BF16, name="w_sb")
+        w_sb = const.tile([P, NJ, DI], BF16, name="w_sb")
 
         def load_w(q):
             nc.sync.dma_start(out=w_sb[:, 2 * q : 2 * q + 2], in_=w_v[:, 2 * q : 2 * q + 2])
@@ -140,24 +140,33 @@ def tile_onebitlinear_t_kernel(
         def w_pe(j):
             wt = psum.tile([P, 512], F32, name="wt", tag="ht", bufs=4)
             for a in range(4):
-                nc.tensor.transpose(wt[:, a * P : (a + 1) * P], w_sb[:, j, a, :].bitcast(F32), ident[:])
+                nc.tensor.transpose(
+                    wt[:, a * P : (a + 1) * P], w_sb[:, j, :].bitcast(F32)[:, a * P : (a + 1) * P], ident[:]
+                )
             xt[("w", j)] = wt
 
         def w_sign(j):
-            src = xt[("w", j)][:].bitcast(BF16).rearrange("p (n g t) -> p n g t", g=2, t=4)
-            dst = wg[:, :, j * P : (j + 1) * P, :].rearrange("p g n t -> p n g t")
-            if j % 2 == 0:
-                nc.scalar.activation(out=dst, in_=src, func=ACT.Sign, bias=sgn_b[:, 0:1], scale=2.0 ** 64)
-            else:
-                nc.vector.tensor_scalar(
-                    out=dst, in0=src, scalar1=0.0, scalar2=2.0, op0=ALU.is_ge, op1=ALU.mult
-                )
+            wv = xt[("w", j)][:].bitcast(BF16)
+            nc.scalar.activation(
+                out=wg[:, 0, j * P : (j + 1) * P, :].rearrange("p n (u e) -> p n u e", u=2),
+                in_=wv[:, 0:512].rearrange("p (u n e) -> p n u e", u=2, e=2),
+                func=ACT.Sign,
+                bias=sgn_b[:, 0:1],
+                scale=2.0 ** 64,
+            )
+            nc.vector.tensor_scalar(
+                out=wg[:, 1, j * P : (j + 1) * P, :].rearrange("p n (u e) -> p n u e", u=2),
+                in0=wv[:, 512:1024].rearrange("p (u n e) -> p n u e", u=2, e=2),
+                scalar1=0.0,
+                scalar2=2.0,
+                op0=ALU.is_ge,
+                op1=ALU.mult,
+            )
 
         def w_quant(q):
-            j = 2 * q + 1
-            odd = wg[:, :, j * P : (j + 1) * P, :].rearrange("p g n t -> p g (n t)")
-            nc.vector.tensor_scalar_add(out=odd, in0=odd, scalar1=-1.0)
             cols = slice(256 * q, 256 * (q + 1))
+            half = wg[:, 1, cols, :].rearrange("p n t -> p (n t)")
+            nc.vector.tensor_scalar_add(out=half, in0=half, scalar1=-1.0)
             for g in range(2):
                 nc.vector.quantize_mx(
                     out=wq[:, g, cols].bitcast(FP8X4),
@@ -166,21 +175,30 @@ def tile_onebitlinear_t_kernel(
                 )
 
         def a_pe(b, qa):
+            g, hh = divmod(qa, 2)
             t = psum.tile([P, 512], F32, name="xtb", tag="xt")
-            for a in range(4):
-                nc.tensor.transpose(
-                    t[:, a * P : (a + 1) * P], x_sb[b][:, 4 * qa + a, :].bitcast(F32), ident[:]
-                )
+            for u in range(2):
+                for cc in range(2):
+                    k0 = (2 * g + u) * P
+                    nc.tensor.transpose(
+                        t[:, (2 * u + cc) * P : (2 * u + cc + 1) * P],
+                        x_sb[b][:, 2 * hh + cc, :].bitcast(F32)[:, k0 : k0 + P],
+                        ident[:],
+                    )
             xt[(b, qa)] = t
 
         def a_v(b, qa):
+            g, hh = divmod(qa, 2)
             if qa == 0:
                 xgt = gpool.tile([P, 2, RB, 4], BF16, name="xgt", align_bytes=64)
                 xg[b] = xgt
             nc.vector.tensor_tensor(
-                out=xg[b][:, :, qa * P : (qa + 1) * P, :].rearrange("p g m t -> p m g t"),
-                in0=xt[(b, qa)][:].bitcast(BF16).rearrange("p (m g t) -> p m g t", g=2, t=4),
-                in1=ics_t.rearrange("p (g t) -> p g t", g=2).unsqueeze(1).to_broadcast([P, P, 2, 4]),
+                out=xg[b][:, g, hh * 256 : (hh + 1) * 256, :].rearrange("p m (u e) -> p m u e", u=2),
+                in0=xt[(b, qa)][:].bitcast(BF16).rearrange("p (u m e) -> p m u e", u=2, e=2),
+                in1=ics_t[:, 4 * g : 4 * g + 4]
+                .rearrange("p (u e) -> p u e", u=2)
+                .unsqueeze(1)
+                .to_broadcast([P, 256, 2, 2]),
                 op=ALU.mult,
             )
 

@@ -47,7 +47,7 @@ def tile_onebitlinear_t_kernel(
         hpool = ctx.enter_context(tc.tile_pool(name="hpool", bufs=2))
         ypool = ctx.enter_context(tc.tile_pool(name="ypool", bufs=5))
         small = ctx.enter_context(tc.tile_pool(name="small", bufs=6))
-        psum = ctx.enter_context(tc.psum_pool(name="psum", bufs=2))
+        psum = ctx.enter_context(tc.psum_pool(name="psum", bufs=8))
         if MANUAL:
             ctx.enter_context(tc.manual_schedule())
 
@@ -95,13 +95,13 @@ def tile_onebitlinear_t_kernel(
         be16 = const.tile([P, DO], BF16, name="be16")
 
         def spread_ics():
-            pt = psum.tile([P, 512], F32, name="pt", tag="ht", bufs=4)
+            pt = psum.tile([P, 512], F32, name="pt", tag="bank")
             nc.tensor.transpose(pt[:, 0:P], vrow[:], ident[:])
             nc.vector.tensor_copy(out=ics_w[:], in_=pt[:, 0:4])
 
         def spread_sb():
             nc.vector.tensor_copy(out=sbf[:], in_=sb16[:])
-            pt = psum.tile([P, 512], F32, name="pt", tag="ht", bufs=4)
+            pt = psum.tile([P, 512], F32, name="pt", tag="bank")
             nc.tensor.transpose(pt[:, 0:P], sbf[:], ident[:])
             nc.vector.tensor_copy(out=sb_t[:], in_=pt[:, 0:16])
 
@@ -109,7 +109,7 @@ def tile_onebitlinear_t_kernel(
             for v, dst in ((0, g16), (1, be16)):
                 for hn in range(2):
                     cols = slice(hn * 512, (hn + 1) * 512)
-                    pt = psum.tile([P, 512], F32, name="pt", tag="ht", bufs=4)
+                    pt = psum.tile([P, 512], F32, name="pt", tag="bank")
                     nc.tensor.matmul(pt[:], lhsT=ones[:], rhs=gz[:, v, cols], start=True, stop=True)
                     nc.scalar.copy(out=dst[:, cols], in_=pt[:])
 
@@ -138,7 +138,7 @@ def tile_onebitlinear_t_kernel(
         wsc = const.tile([P, 2, DO], U8, name="wsc", align_bytes=64)
 
         def w_pe(j):
-            wt = psum.tile([P, 512], F32, name="wt", tag="ht", bufs=4)
+            wt = psum.tile([P, 512], F32, name="wt", tag="bank")
             for a in range(4):
                 nc.tensor.transpose(
                     wt[:, a * P : (a + 1) * P], w_sb[:, j, :].bitcast(F32)[:, a * P : (a + 1) * P], ident[:]
@@ -147,26 +147,17 @@ def tile_onebitlinear_t_kernel(
 
         def w_sign(j):
             wv = xt[("w", j)][:].bitcast(BF16)
-            nc.scalar.activation(
-                out=wg[:, 0, j * P : (j + 1) * P, :].rearrange("p n (u e) -> p n u e", u=2),
-                in_=wv[:, 0:512].rearrange("p (u n e) -> p n u e", u=2, e=2),
-                func=ACT.Sign,
-                bias=sgn_b[:, 0:1],
-                scale=2.0 ** 64,
-            )
-            nc.vector.tensor_scalar(
-                out=wg[:, 1, j * P : (j + 1) * P, :].rearrange("p n (u e) -> p n u e", u=2),
-                in0=wv[:, 512:1024].rearrange("p (u n e) -> p n u e", u=2, e=2),
-                scalar1=0.0,
-                scalar2=2.0,
-                op0=ALU.is_ge,
-                op1=ALU.mult,
-            )
+            for g in range(2):
+                nc.scalar.activation(
+                    out=wg[:, g, j * P : (j + 1) * P, :].rearrange("p n (u e) -> p n u e", u=2),
+                    in_=wv[:, g * 512 : (g + 1) * 512].rearrange("p (u n e) -> p n u e", u=2, e=2),
+                    func=ACT.Sign,
+                    bias=sgn_b[:, 0:1],
+                    scale=2.0 ** 64,
+                )
 
         def w_quant(q):
             cols = slice(256 * q, 256 * (q + 1))
-            half = wg[:, 1, cols, :].rearrange("p n t -> p (n t)")
-            nc.vector.tensor_scalar_add(out=half, in0=half, scalar1=-1.0)
             for g in range(2):
                 nc.vector.quantize_mx(
                     out=wq[:, g, cols].bitcast(FP8X4),
@@ -176,7 +167,7 @@ def tile_onebitlinear_t_kernel(
 
         def a_pe(b, qa):
             g, hh = divmod(qa, 2)
-            t = psum.tile([P, 512], F32, name="xtb", tag="xt")
+            t = psum.tile([P, 512], F32, name="xtb", tag="bank")
             for u in range(2):
                 for cc in range(2):
                     k0 = (2 * g + u) * P
@@ -217,7 +208,7 @@ def tile_onebitlinear_t_kernel(
             if j == 0:
                 hTt = hpool.tile([P, NJ, RB], F32, name="hTt")
                 hT[b] = hTt
-            acc = psum.tile([P, RB], F32, name="acc", tag="acc")
+            acc = psum.tile([P, RB], F32, name="acc", tag="bank")
             for g in range(2):
                 nc.tensor.matmul_mx(
                     out=acc[:],
@@ -238,7 +229,7 @@ def tile_onebitlinear_t_kernel(
 
         def h_pe(b, c):
             for hn in range(2):
-                t = psum.tile([P, 512], F32, name="htb", tag="ht", bufs=4)
+                t = psum.tile([P, 512], F32, name="htb", tag="bank")
                 for jj in range(4):
                     nc.tensor.transpose(
                         t[:, jj * P : (jj + 1) * P],

@@ -31,6 +31,10 @@ def post_kind(b, c):
     return "SG"
 
 
+def stats_on_scalar(b, c):
+    return b % 2 == 1 and c == 1
+
+
 def tile_onebitlinear_t_kernel(
     tc, x, weight, in_channel_scale, out_channel_scale, bias, ln_gamma, ln_beta, out
 ):
@@ -47,6 +51,7 @@ def tile_onebitlinear_t_kernel(
         hpool = ctx.enter_context(tc.tile_pool(name="hpool", bufs=2))
         ypool = ctx.enter_context(tc.tile_pool(name="ypool", bufs=5))
         small = ctx.enter_context(tc.tile_pool(name="small", bufs=6))
+        jpool = ctx.enter_context(tc.tile_pool(name="jpool", bufs=2))
         psum = ctx.enter_context(tc.psum_pool(name="psum", bufs=8))
         if MANUAL:
             ctx.enter_context(tc.manual_schedule())
@@ -238,13 +243,42 @@ def tile_onebitlinear_t_kernel(
                     )
                 ht[(b, c, hn)] = t
 
+        def h_st_scalar(b, c):
+            sums = small.tile([P, 2], F32, name="sums")
+            for hn in range(2):
+                junk = jpool.tile([P, 512], BF16, name="junk")
+                nc.scalar.activation(
+                    out=junk[:], in_=ht[(b, c, hn)][:], func=ACT.Identity, accum_out=sums[:, hn : hn + 1]
+                )
+            nm = small.tile([P, 1], F32, name="nm")
+            j2 = small.tile([P, 2], F32, name="j2")
+            nc.scalar.activation(out=j2[:], in_=sums[:], func=ACT.Copy, scale=-1.0 / DO, accum_out=nm[:, 0:1])
+            ss = small.tile([P, 2], F32, name="ss")
+            for hn in range(2):
+                junk = jpool.tile([P, 512], BF16, name="junk")
+                nc.scalar.activation(
+                    out=junk[:],
+                    in_=ht[(b, c, hn)][:],
+                    func=ACT.Square,
+                    bias=nm[:, 0:1],
+                    scale=1.0,
+                    accum_out=ss[:, hn : hn + 1],
+                )
+            var = small.tile([P, 1], F32, name="var")
+            j3 = small.tile([P, 2], F32, name="j3")
+            nc.scalar.activation(out=j3[:], in_=ss[:], func=ACT.Copy, scale=1.0 / DO, accum_out=var[:, 0:1])
+            mvs[(b, c)] = (nm, var)
+
         def h_st(b, c):
+            if stats_on_scalar(b, c):
+                h_st_scalar(b, c)
+                return
             st = small.tile([P, 2, 6], F32, name="st")
             for hn in range(2):
                 nc.vector.bn_stats(out=st[:, hn, :], in_=ht[(b, c, hn)][:])
             mv = small.tile([P, 2], F32, name="mv")
             nc.vector.bn_aggr(out=mv[:], in_=st[:].rearrange("p h s -> p (h s)"))
-            mvs[(b, c)] = mv
+            mvs[(b, c)] = (mv[:, 0:1], mv[:, 1:2])
 
         def h_b(b, c):
             y = ypool.tile([P, DO], F32, name="y")
@@ -253,9 +287,9 @@ def tile_onebitlinear_t_kernel(
                 nc.vector.scalar_tensor_tensor(
                     out=y[:, hn * 512 : (hn + 1) * 512],
                     in0=ht[(b, c, hn)][:],
-                    scalar=mvs[(b, c)][:, 0:1],
+                    scalar=mvs[(b, c)][0][:, 0:1],
                     in1=g16[:, hn * 512 : (hn + 1) * 512],
-                    op0=ALU.subtract,
+                    op0=ALU.add if stats_on_scalar(b, c) else ALU.subtract,
                     op1=ALU.mult,
                 )
 
@@ -263,7 +297,7 @@ def tile_onebitlinear_t_kernel(
             rs = small.tile([P, 1], F32, name="rs")
             nc.scalar.activation(
                 out=rs[:],
-                in_=mvs[(b, c)][:, 1:2],
+                in_=mvs[(b, c)][1][:, 0:1],
                 func=ACT.Abs_reciprocal_sqrt,
                 bias=eps_t[:, 0:1],
                 scale=1.0,

@@ -17,22 +17,21 @@ DI = 1024
 DO = 1024
 RB = 512
 NB = R // RB
+NT = R // P
 NJ = DO // P
 LN_EPS = 1e-5
 FLOPS = 2 * R * DI * DO
 
-MANUAL = False
-XS_BUFS = 3
+LATE = 21
+AHEAD = 11
 
 
-def post_kind(b, c):
-    if b == NB - 1 and c == 3:
+def post_kind(i):
+    if i >= NT - 2:
         return "V"
-    return "SG"
-
-
-def stats_on_scalar(b, c):
-    return b % 2 == 1 and c == 1
+    if i < 18 and i % 3 == 1:
+        return "G"
+    return "S"
 
 
 def tile_onebitlinear_t_kernel(
@@ -45,35 +44,39 @@ def tile_onebitlinear_t_kernel(
 
     with ExitStack() as ctx:
         const = ctx.enter_context(tc.tile_pool(name="const", bufs=1))
-        xpool = ctx.enter_context(tc.tile_pool(name="xpool", bufs=XS_BUFS))
-        gpool = ctx.enter_context(tc.tile_pool(name="gpool", bufs=2))
-        qpool = ctx.enter_context(tc.tile_pool(name="qpool", bufs=2))
+        xpool = ctx.enter_context(tc.tile_pool(name="xpool", bufs=NB))
+        gpool = ctx.enter_context(tc.tile_pool(name="gpool", bufs=3))
+        qpool = ctx.enter_context(tc.tile_pool(name="qpool", bufs=4))
         hpool = ctx.enter_context(tc.tile_pool(name="hpool", bufs=2))
-        ypool = ctx.enter_context(tc.tile_pool(name="ypool", bufs=5))
+        ypool = ctx.enter_context(tc.tile_pool(name="ypool", bufs=8))
         small = ctx.enter_context(tc.tile_pool(name="small", bufs=6))
-        jpool = ctx.enter_context(tc.tile_pool(name="jpool", bufs=2))
-        psum = ctx.enter_context(tc.psum_pool(name="psum", bufs=8))
-        if MANUAL:
-            ctx.enter_context(tc.manual_schedule())
+        psum_x = ctx.enter_context(tc.psum_pool(name="psum_x", bufs=2))
+        psum_m = ctx.enter_context(tc.psum_pool(name="psum_m", bufs=2))
+        psum_h = ctx.enter_context(tc.psum_pool(name="psum_h", bufs=4))
+        ctx.enter_context(tc.manual_schedule())
 
         x_sb = {}
         xg = {}
         xq = {}
         xsc = {}
         xt = {}
+        wt = {}
         hT = {}
         ht = {}
         yt = {}
         mvs = {}
         rstds = {}
+        nmrs = {}
 
         def load_x(b):
             xs = xpool.tile([P, 4, DI], BF16, name="xs")
-            parts = 2 if b == 0 else 1
-            for i in range(parts):
-                ts = slice(i * 4 // parts, (i + 1) * 4 // parts)
-                nc.sync.dma_start(out=xs[:, ts, :], in_=x_blk[b][:, ts, :])
             x_sb[b] = xs
+            if b == 0:
+                nc.sync.dma_start(out=xs[:, 0:2, :], in_=x_blk[b][:, 0:2, :])
+                load_w(0)
+                nc.sync.dma_start(out=xs[:, 2:4, :], in_=x_blk[b][:, 2:4, :])
+            else:
+                nc.sync.dma_start(out=xs[:], in_=x_blk[b])
 
         ident = const.tile([P, P], F32, name="ident")
         make_identity(nc, ident[:])
@@ -85,6 +88,10 @@ def tile_onebitlinear_t_kernel(
         nc.vector.memset(gz[:], 0.0)
         ones = const.tile([P, P], BF16, name="ones")
         nc.vector.memset(ones[:], 1.0)
+        eps_t = const.tile([P, 1], F32, name="eps_t")
+        nc.vector.memset(eps_t[:], LN_EPS)
+        sgn_b = const.tile([P, 1], F32, name="sgn_b")
+        nc.vector.memset(sgn_b[:], 2.0 ** -80)
         nc.scalar.dma_start(
             out=vrow[0:4, :].bitcast(BF16), in_=in_channel_scale.rearrange("(a k) -> a k", a=4)
         )
@@ -96,62 +103,52 @@ def tile_onebitlinear_t_kernel(
         ics_t = ics_w[:].bitcast(BF16)
         sbf = const.tile([P, P], F32, name="sbf")
         sb_t = const.tile([P, 16], F32, name="sb_t")
-        g16 = const.tile([P, DO], BF16, name="g16")
-        be16 = const.tile([P, DO], BF16, name="be16")
-
-        def spread_ics():
-            pt = psum.tile([P, 512], F32, name="pt", tag="bank")
-            nc.tensor.transpose(pt[:, 0:P], vrow[:], ident[:])
-            nc.vector.tensor_copy(out=ics_w[:], in_=pt[:, 0:4])
-
-        def spread_sb():
-            nc.vector.tensor_copy(out=sbf[:], in_=sb16[:])
-            pt = psum.tile([P, 512], F32, name="pt", tag="bank")
-            nc.tensor.transpose(pt[:, 0:P], sbf[:], ident[:])
-            nc.vector.tensor_copy(out=sb_t[:], in_=pt[:, 0:16])
-
-        def spread_gb():
-            for v, dst in ((0, g16), (1, be16)):
-                for hn in range(2):
-                    cols = slice(hn * 512, (hn + 1) * 512)
-                    pt = psum.tile([P, 512], F32, name="pt", tag="bank")
-                    nc.tensor.matmul(pt[:], lhsT=ones[:], rhs=gz[:, v, cols], start=True, stop=True)
-                    nc.scalar.copy(out=dst[:, cols], in_=pt[:])
-
+        s_t = sb_t[:, 0:NJ]
+        b_t = sb_t[:, NJ : 2 * NJ]
+        gb16 = const.tile([P, 2, DO], BF16, name="gb16")
         w_sb = const.tile([P, NJ, DI], BF16, name="w_sb")
+        wg = const.tile([P, 2, DO, 4], BF16, name="wg", align_bytes=64)
+        wq = const.tile([P, 2, DO], U32, name="wq", align_bytes=64)
+        wsc = const.tile([P, 2, DO], U8, name="wsc", align_bytes=64)
 
         def load_w(q):
             nc.sync.dma_start(out=w_sb[:, 2 * q : 2 * q + 2], in_=w_v[:, 2 * q : 2 * q + 2])
 
         load_x(0)
-        load_w(0)
-        load_w(1)
-        load_x(1)
-        load_w(2)
-        load_w(3)
-        load_x(2)
+        for q in range(1, 4):
+            load_w(q)
+        for b in range(1, NB):
+            load_x(b)
 
-        s_t = sb_t[:, 0:NJ]
-        b_t = sb_t[:, NJ : 2 * NJ]
-        eps_t = const.tile([P, 1], F32, name="eps_t")
-        nc.vector.memset(eps_t[:], LN_EPS)
-        sgn_b = const.tile([P, 1], F32, name="sgn_b")
-        nc.vector.memset(sgn_b[:], 2.0 ** -80)
+        def spread_ics():
+            pt = psum_h.tile([P, 512], F32, name="pt", tag="hb")
+            nc.tensor.transpose(pt[:, 0:P], vrow[:], ident[:])
+            nc.vector.tensor_copy(out=ics_w[:], in_=pt[:, 0:4])
 
-        wg = const.tile([P, 2, DO, 4], BF16, name="wg", align_bytes=64)
-        wq = const.tile([P, 2, DO], U32, name="wq", align_bytes=64)
-        wsc = const.tile([P, 2, DO], U8, name="wsc", align_bytes=64)
+        def spread_sb():
+            nc.vector.tensor_copy(out=sbf[:], in_=sb16[:])
+            pt = psum_h.tile([P, 512], F32, name="pt", tag="hb")
+            nc.tensor.transpose(pt[:, 0:P], sbf[:], ident[:])
+            nc.vector.tensor_copy(out=sb_t[:], in_=pt[:, 0:16])
+
+        def spread_gb():
+            for v in range(2):
+                pt = psum_h.tile([P, DO], BF16, name="ptb", tag="hb")
+                for hn in range(2):
+                    cols = slice(hn * 512, (hn + 1) * 512)
+                    nc.tensor.matmul(pt[:, cols], lhsT=ones[:], rhs=gz[:, v, cols], start=True, stop=True)
+                nc.scalar.copy(out=gb16[:, v, :], in_=pt[:])
 
         def w_pe(j):
-            wt = psum.tile([P, 512], F32, name="wt", tag="bank")
+            t = psum_h.tile([P, 512], F32, name="wt", tag="hb")
             for a in range(4):
                 nc.tensor.transpose(
-                    wt[:, a * P : (a + 1) * P], w_sb[:, j, :].bitcast(F32)[:, a * P : (a + 1) * P], ident[:]
+                    t[:, a * P : (a + 1) * P], w_sb[:, j, :].bitcast(F32)[:, a * P : (a + 1) * P], ident[:]
                 )
-            xt[("w", j)] = wt
+            wt[j] = t
 
         def w_sign(j):
-            wv = xt[("w", j)][:].bitcast(BF16)
+            wv = wt[j][:].bitcast(BF16)
             for g in range(2):
                 nc.scalar.activation(
                     out=wg[:, g, j * P : (j + 1) * P, :].rearrange("p n (u e) -> p n u e", u=2),
@@ -159,6 +156,24 @@ def tile_onebitlinear_t_kernel(
                     func=ACT.Sign,
                     bias=sgn_b[:, 0:1],
                     scale=2.0 ** 64,
+                )
+
+        def w_ge(q):
+            wv = w_sb[:, 2 * q : 2 * q + 2, :].rearrange("p j k -> p (j k)")
+            nc.vector.tensor_scalar(out=wv, in0=wv, scalar1=0.0, scalar2=2.0, op0=ALU.is_ge, op1=ALU.mult)
+
+        def w_pm(q):
+            wv = w_sb[:, 2 * q : 2 * q + 2, :].rearrange("p j k -> p (j k)")
+            nc.vector.tensor_scalar(out=wv, in0=wv, scalar1=1.0, scalar2=-1.0, op0=ALU.mult, op1=ALU.add)
+
+        def w_copy(j):
+            for g in range(2):
+                nc.scalar.copy(
+                    out=wg[:, g, j * P : (j + 1) * P, :]
+                    .rearrange("p n t -> p (n t)")
+                    .bitcast(F32)
+                    .rearrange("p (n u) -> p n u", u=2),
+                    in_=wt[j][:, g * 256 : (g + 1) * 256].rearrange("p (u n) -> p n u", u=2),
                 )
 
         def w_quant(q):
@@ -170,9 +185,10 @@ def tile_onebitlinear_t_kernel(
                     in_=wg[:, g, cols, :].rearrange("p n t -> p (n t)"),
                 )
 
-        def a_pe(b, qa):
-            g, hh = divmod(qa, 2)
-            t = psum.tile([P, 512], F32, name="xtb", tag="bank")
+        def x_pe(n):
+            b, q = divmod(n, 4)
+            hh, g = divmod(q, 2)
+            t = psum_x.tile([P, 512], F32, name="xtb", tag="xtb")
             for u in range(2):
                 for cc in range(2):
                     k0 = (2 * g + u) * P
@@ -181,16 +197,17 @@ def tile_onebitlinear_t_kernel(
                         x_sb[b][:, 2 * hh + cc, :].bitcast(F32)[:, k0 : k0 + P],
                         ident[:],
                     )
-            xt[(b, qa)] = t
+            xt[n] = t
 
-        def a_v(b, qa):
-            g, hh = divmod(qa, 2)
-            if qa == 0:
+        def x_v(n):
+            b, q = divmod(n, 4)
+            hh, g = divmod(q, 2)
+            if q == 0:
                 xgt = gpool.tile([P, 2, RB, 4], BF16, name="xgt", align_bytes=64)
                 xg[b] = xgt
             nc.vector.tensor_tensor(
                 out=xg[b][:, g, hh * 256 : (hh + 1) * 256, :].rearrange("p m (u e) -> p m u e", u=2),
-                in0=xt[(b, qa)][:].bitcast(BF16).rearrange("p (u m e) -> p m u e", u=2, e=2),
+                in0=xt[n][:].bitcast(BF16).rearrange("p (u m e) -> p m u e", u=2, e=2),
                 in1=ics_t[:, 4 * g : 4 * g + 4]
                 .rearrange("p (u e) -> p u e", u=2)
                 .unsqueeze(1)
@@ -198,180 +215,244 @@ def tile_onebitlinear_t_kernel(
                 op=ALU.mult,
             )
 
-        def a_quant(b):
-            xqt = qpool.tile([P, 2, RB], U32, name="xqt", align_bytes=64)
-            xst = qpool.tile([P, 2, RB], U8, name="xst", align_bytes=64)
-            xq[b] = xqt
-            xsc[b] = xst
+        def x_q(n):
+            b, q = divmod(n, 4)
+            hh, g = divmod(q, 2)
+            if q == 0:
+                xqt = qpool.tile([P, 2, RB], U32, name="xqt", align_bytes=64)
+                xst = qpool.tile([P, 2, RB], U8, name="xst", align_bytes=64)
+                xq[b] = xqt
+                xsc[b] = xst
+            rows = slice(hh * 256, (hh + 1) * 256)
             nc.vector.quantize_mx(
-                out=xqt[:].rearrange("p g m -> p (g m)").bitcast(FP8X4),
-                scales=xst[:].rearrange("p g m -> p (g m)"),
-                in_=xg[b][:].rearrange("p g m t -> p (g m t)"),
+                out=xq[b][:, g, rows].bitcast(FP8X4),
+                scales=xsc[b][:, g, rows],
+                in_=xg[b][:, g, rows, :].rearrange("p m t -> p (m t)"),
             )
 
-        def m_tile(b, j):
-            if j == 0:
+        accs = {}
+
+        def mx(t):
+            b, q = divmod(t, 4)
+            for j in (2 * q, 2 * q + 1):
+                acc = psum_m.tile([P, RB], F32, name="acc")
+                accs[(b, j)] = acc
+                for g in range(2):
+                    nc.tensor.matmul_mx(
+                        out=acc[:],
+                        lhsT=wq[:, g, j * P : (j + 1) * P].bitcast(FP8X4),
+                        lhsT_scale=wsc[:, g, j * P : (j + 1) * P],
+                        rhs=xq[b][:, g, :].bitcast(FP8X4),
+                        rhs_scale=xsc[b][:, g, :],
+                        start=(g == 0),
+                        stop=(g == 1),
+                    )
+
+        def exits(t):
+            b, q = divmod(t, 4)
+            if q == 0:
                 hTt = hpool.tile([P, NJ, RB], F32, name="hTt")
                 hT[b] = hTt
-            acc = psum.tile([P, RB], F32, name="acc", tag="bank")
-            for g in range(2):
-                nc.tensor.matmul_mx(
-                    out=acc[:],
-                    lhsT=wq[:, g, j * P : (j + 1) * P].bitcast(FP8X4),
-                    lhsT_scale=wsc[:, g, j * P : (j + 1) * P],
-                    rhs=xq[b][:, g, :].bitcast(FP8X4),
-                    rhs_scale=xsc[b][:, g, :],
-                    start=(g == 0),
-                    stop=(g == 1),
+            for j in (2 * q, 2 * q + 1):
+                nc.scalar.activation(
+                    out=hT[b][:, j, :],
+                    in_=accs[(b, j)][:],
+                    func=ACT.Identity,
+                    bias=b_t[:, j : j + 1],
+                    scale=s_t[:, j : j + 1],
                 )
-            nc.scalar.activation(
-                out=hT[b][:, j, :],
-                in_=acc[:],
-                func=ACT.Identity,
-                bias=b_t[:, j : j + 1],
-                scale=s_t[:, j : j + 1],
-            )
 
-        def h_pe(b, c):
+        def h_pe(i):
+            b, c = divmod(i, 4)
             for hn in range(2):
-                t = psum.tile([P, 512], F32, name="htb", tag="bank")
+                pool, tag = (psum_x, "xtb") if i >= LATE and i % 3 == 0 else (psum_h, "hb")
+                t = pool.tile([P, 512], F32, name="htb", tag=tag)
                 for jj in range(4):
                     nc.tensor.transpose(
                         t[:, jj * P : (jj + 1) * P],
                         hT[b][:, 4 * hn + jj, c * P : (c + 1) * P],
                         ident[:],
                     )
-                ht[(b, c, hn)] = t
+                ht[(i, hn)] = t
 
-        def h_st_scalar(b, c):
-            sums = small.tile([P, 2], F32, name="sums")
-            for hn in range(2):
-                junk = jpool.tile([P, 512], BF16, name="junk")
-                nc.scalar.activation(
-                    out=junk[:], in_=ht[(b, c, hn)][:], func=ACT.Identity, accum_out=sums[:, hn : hn + 1]
-                )
-            nm = small.tile([P, 1], F32, name="nm")
-            j2 = small.tile([P, 2], F32, name="j2")
-            nc.scalar.activation(out=j2[:], in_=sums[:], func=ACT.Copy, scale=-1.0 / DO, accum_out=nm[:, 0:1])
-            ss = small.tile([P, 2], F32, name="ss")
-            for hn in range(2):
-                junk = jpool.tile([P, 512], BF16, name="junk")
-                nc.scalar.activation(
-                    out=junk[:],
-                    in_=ht[(b, c, hn)][:],
-                    func=ACT.Square,
-                    bias=nm[:, 0:1],
-                    scale=1.0,
-                    accum_out=ss[:, hn : hn + 1],
-                )
-            var = small.tile([P, 1], F32, name="var")
-            j3 = small.tile([P, 2], F32, name="j3")
-            nc.scalar.activation(out=j3[:], in_=ss[:], func=ACT.Copy, scale=1.0 / DO, accum_out=var[:, 0:1])
-            mvs[(b, c)] = (nm, var)
+        sts = {}
 
-        def h_st(b, c):
-            if stats_on_scalar(b, c):
-                h_st_scalar(b, c)
-                return
-            st = small.tile([P, 2, 6], F32, name="st")
-            for hn in range(2):
-                nc.vector.bn_stats(out=st[:, hn, :], in_=ht[(b, c, hn)][:])
+        def bn(i, hn):
+            if hn == 0:
+                st = small.tile([P, 2, 6], F32, name="st")
+                sts[i] = st
+            nc.vector.bn_stats(out=sts[i][:, hn, :], in_=ht[(i, hn)][:])
+
+        def aggr(i):
             mv = small.tile([P, 2], F32, name="mv")
-            nc.vector.bn_aggr(out=mv[:], in_=st[:].rearrange("p h s -> p (h s)"))
-            mvs[(b, c)] = (mv[:, 0:1], mv[:, 1:2])
+            nc.vector.bn_aggr(out=mv[:], in_=sts[i][:].rearrange("p h s -> p (h s)"))
+            mvs[i] = mv
 
-        def h_b(b, c):
+        def stt(i):
             y = ypool.tile([P, DO], F32, name="y")
-            yt[(b, c)] = y
+            yt[i] = y
             for hn in range(2):
+                cols = slice(hn * 512, (hn + 1) * 512)
                 nc.vector.scalar_tensor_tensor(
-                    out=y[:, hn * 512 : (hn + 1) * 512],
-                    in0=ht[(b, c, hn)][:],
-                    scalar=mvs[(b, c)][0][:, 0:1],
-                    in1=g16[:, hn * 512 : (hn + 1) * 512],
-                    op0=ALU.add if stats_on_scalar(b, c) else ALU.subtract,
+                    out=y[:, cols],
+                    in0=ht[(i, hn)][:],
+                    scalar=mvs[i][:, 0:1],
+                    in1=gb16[:, 0, cols],
+                    op0=ALU.subtract,
                     op1=ALU.mult,
                 )
 
-        def h_rs(b, c):
+        def rs_s(i):
             rs = small.tile([P, 1], F32, name="rs")
             nc.scalar.activation(
                 out=rs[:],
-                in_=mvs[(b, c)][1][:, 0:1],
+                in_=mvs[i][:, 1:2],
                 func=ACT.Abs_reciprocal_sqrt,
                 bias=eps_t[:, 0:1],
                 scale=1.0,
             )
-            rstds[(b, c)] = rs
+            rstds[i] = rs
 
-        def h_s(b, c):
-            y = yt[(b, c)]
-            if post_kind(b, c) == "V":
+        def nmr_v(i):
+            nmr = small.tile([P, 1], F32, name="nmr")
+            nc.vector.tensor_scalar(
+                out=nmr[:], in0=mvs[i][:, 0:1], scalar1=rstds[i][:, 0:1], scalar2=-1.0, op0=ALU.mult, op1=ALU.mult
+            )
+            nmrs[i] = nmr
+
+        def scale_s(i):
+            kind = post_kind(i)
+            if kind == "S":
+                y = yt[i]
+                nc.scalar.activation(out=y[:], in_=y[:], func=ACT.Copy, scale=rstds[i][:, 0:1])
+            elif kind == "G":
+                y = ypool.tile([P, DO], F32, name="y")
+                yt[i] = y
+                for hn in range(2):
+                    nc.scalar.activation(
+                        out=y[:, hn * 512 : (hn + 1) * 512],
+                        in_=ht[(i, hn)][:],
+                        func=ACT.Identity,
+                        bias=nmrs[i][:, 0:1],
+                        scale=rstds[i][:, 0:1],
+                    )
+
+        def fin(i):
+            b, c = divmod(i, 4)
+            kind = post_kind(i)
+            y = yt[i]
+            if kind == "V":
                 for hn in range(2):
                     cols = slice(hn * 512, (hn + 1) * 512)
                     nc.vector.scalar_tensor_tensor(
                         out=y[:, cols],
                         in0=y[:, cols],
-                        scalar=rstds[(b, c)][:, 0:1],
-                        in1=be16[:, cols],
+                        scalar=rstds[i][:, 0:1],
+                        in1=gb16[:, 1, cols],
                         op0=ALU.mult,
                         op1=ALU.add,
                     )
                     nc.sync.dma_start(out=o_blk[b, c][:, cols], in_=y[:, cols])
-            else:
-                nc.scalar.activation(out=y[:], in_=y[:], func=ACT.Copy, scale=rstds[(b, c)][:, 0:1])
-
-        def h_g(b, c):
-            if post_kind(b, c) == "V":
                 return
-            y = yt[(b, c)]
-            nc.gpsimd.tensor_tensor(out=y[:], in0=y[:], in1=be16[:], op=ALU.add)
+            if kind == "G":
+                nc.gpsimd.tensor_tensor(out=y[:], in0=y[:], in1=gb16[:, 0, :], op=ALU.mult)
+            nc.gpsimd.tensor_tensor(out=y[:], in0=y[:], in1=gb16[:, 1, :], op=ALU.add)
             nc.sync.dma_start(out=o_blk[b, c], in_=y[:])
 
-        def at(t, off):
-            b, q = divmod(t - off, 4)
-            if 0 <= b < NB:
-                return b, q
-            return None
-
         spread_ics()
-        for t in range(-6, 4 * NB + 11):
-            e = at(t, -5)
-            if e:
-                a_v(e[0], e[1])
-            e = at(t, -6)
-            if e:
-                a_pe(e[0], e[1])
-            if -4 <= t < 0:
-                for j in (2 * (t + 4), 2 * (t + 4) + 1):
-                    w_pe(j)
-                    w_sign(j)
-            e = at(t, 0)
-            if e:
-                m_tile(e[0], 2 * e[1])
-                m_tile(e[0], 2 * e[1] + 1)
-            e = at(t, 4)
-            if e:
-                h_pe(e[0], e[1])
-            e = at(t, 5)
-            if e:
-                h_st(e[0], e[1])
-                h_rs(e[0], e[1])
-                h_b(e[0], e[1])
-            e = at(t, 6)
-            if e:
-                h_s(e[0], e[1])
-            e = at(t, 7)
-            if e:
-                h_g(e[0], e[1])
-            if -3 <= t < 1:
-                w_quant(t + 3)
-            if t == -1:
-                spread_sb()
-                spread_gb()
-            e = at(t, -1)
-            if e and e[1] == 0:
-                a_quant(e[0])
-            e = at(t, -13)
-            if e and e[1] == 0 and e[0] >= XS_BUFS:
-                load_x(e[0])
+        for n in range(2):
+            x_pe(n)
+            x_v(n)
+        for j in range(2):
+            w_pe(j)
+            w_sign(j)
+        for n in range(2, 4):
+            x_pe(n)
+            x_v(n)
+        for j in range(2, 4):
+            w_pe(j)
+            w_sign(j)
+        spread_sb()
+        w_ge(2)
+        x_q(0)
+        x_q(1)
+        w_pm(2)
+        w_ge(3)
+        x_q(2)
+        x_q(3)
+        w_pm(3)
+        for j in (4, 5):
+            w_pe(j)
+            w_copy(j)
+        w_quant(0)
+        x_pe(4)
+        x_pe(5)
+        for j in (6, 7):
+            w_pe(j)
+            w_copy(j)
+        mx(0)
+        exits(0)
+        w_quant(1)
+        x_v(4)
+        x_v(5)
+        w_quant(2)
+        mx(1)
+        exits(1)
+        x_pe(6)
+        w_quant(3)
+        x_v(6)
+        x_pe(7)
+        x_v(7)
+        mx(2)
+        exits(2)
+        x_q(4)
+        x_q(5)
+        x_pe(8)
+        x_v(8)
+        x_q(6)
+        x_q(7)
+        mx(3)
+        exits(3)
+        x_pe(9)
+        x_v(9)
+        spread_gb()
+        x_pe(10)
+        x_v(10)
+        x_q(8)
+        x_q(9)
+
+        h_pe(0)
+        for t in range(4, NT + 6):
+            i = t - 4
+            n = AHEAD + i
+            if t < NT:
+                mx(t)
+                exits(t)
+            if n < 4 * NB:
+                x_pe(n)
+            if i + 1 < NT:
+                h_pe(i + 1)
+            if i < NT:
+                bn(i, 0)
+            if 0 <= i - 1 < LATE:
+                if post_kind(i - 1) == "G":
+                    nmr_v(i - 1)
+                scale_s(i - 1)
+            if i < NT:
+                bn(i, 1)
+            if n < 4 * NB:
+                x_v(n)
+            if i - 1 >= LATE and i - 1 < NT:
+                stt(i - 1)
+            if i < NT:
+                aggr(i)
+                rs_s(i)
+            if n - 1 < 4 * NB:
+                x_q(n - 1)
+            if i < LATE and post_kind(i) != "G":
+                stt(i)
+            if 0 <= i - 1 < LATE:
+                fin(i - 1)
+            if i - 2 >= LATE and i - 2 < NT:
+                scale_s(i - 2)
+                fin(i - 2)

@@ -22,14 +22,17 @@ NJ = DO // P
 LN_EPS = 1e-5
 FLOPS = 2 * R * DI * DO
 
-LATE = 21
-AHEAD = 11
+AHEAD = 10
+
+
+def half_on_scalar(i):
+    return False
 
 
 def post_kind(i):
     if i >= NT - 2:
         return "V"
-    if i < 18 and i % 3 == 1:
+    if i < 20 and i % 3 == 1:
         return "G"
     return "S"
 
@@ -50,6 +53,7 @@ def tile_onebitlinear_t_kernel(
         hpool = ctx.enter_context(tc.tile_pool(name="hpool", bufs=2))
         ypool = ctx.enter_context(tc.tile_pool(name="ypool", bufs=8))
         small = ctx.enter_context(tc.tile_pool(name="small", bufs=6))
+        jpool = ctx.enter_context(tc.tile_pool(name="jpool", bufs=2))
         psum_x = ctx.enter_context(tc.psum_pool(name="psum_x", bufs=2))
         psum_m = ctx.enter_context(tc.psum_pool(name="psum_m", bufs=2))
         psum_h = ctx.enter_context(tc.psum_pool(name="psum_h", bufs=4))
@@ -215,19 +219,15 @@ def tile_onebitlinear_t_kernel(
                 op=ALU.mult,
             )
 
-        def x_q(n):
-            b, q = divmod(n, 4)
-            hh, g = divmod(q, 2)
-            if q == 0:
-                xqt = qpool.tile([P, 2, RB], U32, name="xqt", align_bytes=64)
-                xst = qpool.tile([P, 2, RB], U8, name="xst", align_bytes=64)
-                xq[b] = xqt
-                xsc[b] = xst
-            rows = slice(hh * 256, (hh + 1) * 256)
+        def x_q(b):
+            xqt = qpool.tile([P, 2, RB], U32, name="xqt", align_bytes=64)
+            xst = qpool.tile([P, 2, RB], U8, name="xst", align_bytes=64)
+            xq[b] = xqt
+            xsc[b] = xst
             nc.vector.quantize_mx(
-                out=xq[b][:, g, rows].bitcast(FP8X4),
-                scales=xsc[b][:, g, rows],
-                in_=xg[b][:, g, rows, :].rearrange("p m t -> p (m t)"),
+                out=xqt[:].rearrange("p g m -> p (g m)").bitcast(FP8X4),
+                scales=xst[:].rearrange("p g m -> p (g m)"),
+                in_=xg[b][:].rearrange("p g m t -> p (g m t)"),
             )
 
         accs = {}
@@ -262,11 +262,10 @@ def tile_onebitlinear_t_kernel(
                     scale=s_t[:, j : j + 1],
                 )
 
-        def h_pe(i):
+        def h_pe(i, hns=(0, 1)):
             b, c = divmod(i, 4)
-            for hn in range(2):
-                pool, tag = (psum_x, "xtb") if i >= LATE and i % 3 == 0 else (psum_h, "hb")
-                t = pool.tile([P, 512], F32, name="htb", tag=tag)
+            for hn in hns:
+                t = psum_h.tile([P, 512], F32, name="htb", tag="hb")
                 for jj in range(4):
                     nc.tensor.transpose(
                         t[:, jj * P : (jj + 1) * P],
@@ -277,30 +276,59 @@ def tile_onebitlinear_t_kernel(
 
         sts = {}
 
+        sth = []
+        for n in range(4):
+            st = const.tile([P, 9], F32, name=f"sth{n}")
+            nc.gpsimd.memset(st[:], 512.0)
+            sth.append(st)
+
         def bn(i, hn):
             if hn == 0:
-                st = small.tile([P, 2, 6], F32, name="st")
+                if half_on_scalar(i):
+                    st = sth[i % 4]
+                else:
+                    st = small.tile([P, 12], F32, name="st")
                 sts[i] = st
-            nc.vector.bn_stats(out=sts[i][:, hn, :], in_=ht[(i, hn)][:])
+            elif half_on_scalar(i):
+                return
+            nc.vector.bn_stats(out=sts[i][:, 6 * hn : 6 * hn + 6], in_=ht[(i, hn)][:])
+
+        def bn_s(i):
+            st = sth[i % 4]
+            junk = jpool.tile([P, 512], BF16, name="junk")
+            nc.scalar.activation(
+                out=junk[:], in_=ht[(i, 1)][:], func=ACT.Identity, scale=1.0 / 512, accum_out=st[:, 7:8]
+            )
+            junk = jpool.tile([P, 512], BF16, name="junk")
+            nc.scalar.activation(
+                out=junk[:],
+                in_=ht[(i, 1)][:],
+                func=ACT.Square,
+                bias=st[:, 7:8],
+                scale=-1.0,
+                accum_out=st[:, 8:9],
+            )
 
         def aggr(i):
             mv = small.tile([P, 2], F32, name="mv")
-            nc.vector.bn_aggr(out=mv[:], in_=sts[i][:].rearrange("p h s -> p (h s)"))
+            nc.vector.bn_aggr(out=mv[:], in_=sts[i][:, 0 : 9 if half_on_scalar(i) else 12])
             mvs[i] = mv
 
-        def stt(i):
-            y = ypool.tile([P, DO], F32, name="y")
-            yt[i] = y
-            for hn in range(2):
-                cols = slice(hn * 512, (hn + 1) * 512)
-                nc.vector.scalar_tensor_tensor(
-                    out=y[:, cols],
-                    in0=ht[(i, hn)][:],
-                    scalar=mvs[i][:, 0:1],
-                    in1=gb16[:, 0, cols],
-                    op0=ALU.subtract,
-                    op1=ALU.mult,
-                )
+        def stt(i, hn):
+            if post_kind(i) == "G":
+                return
+            if hn == 0:
+                y = ypool.tile([P, DO], F32, name="y")
+                yt[i] = y
+            cols = slice(hn * 512, (hn + 1) * 512)
+            nc.vector.scalar_tensor_tensor(
+                out=yt[i][:, cols],
+                in0=ht[(i, hn)][:],
+                scalar=mvs[i][:, 0:1],
+                in1=gb16[:, 0, cols],
+                op0=ALU.subtract,
+                op1=ALU.mult,
+            )
 
         def rs_s(i):
             rs = small.tile([P, 1], F32, name="rs")
@@ -313,11 +341,11 @@ def tile_onebitlinear_t_kernel(
             )
             rstds[i] = rs
 
-        def nmr_v(i):
+        def nmr_s(i):
+            nrs = small.tile([P, 1], F32, name="nrs")
+            nc.scalar.activation(out=nrs[:], in_=rstds[i][:], func=ACT.Copy, scale=-1.0)
             nmr = small.tile([P, 1], F32, name="nmr")
-            nc.vector.tensor_scalar(
-                out=nmr[:], in0=mvs[i][:, 0:1], scalar1=rstds[i][:, 0:1], scalar2=-1.0, op0=ALU.mult, op1=ALU.mult
-            )
+            nc.scalar.activation(out=nmr[:], in_=mvs[i][:, 0:1], func=ACT.Copy, scale=nrs[:, 0:1])
             nmrs[i] = nmr
 
         def scale_s(i):
@@ -374,12 +402,9 @@ def tile_onebitlinear_t_kernel(
             w_sign(j)
         spread_sb()
         w_ge(2)
-        x_q(0)
-        x_q(1)
-        w_pm(2)
         w_ge(3)
-        x_q(2)
-        x_q(3)
+        w_pm(2)
+        x_q(0)
         w_pm(3)
         for j in (4, 5):
             w_pe(j)
@@ -395,64 +420,58 @@ def tile_onebitlinear_t_kernel(
         w_quant(1)
         x_v(4)
         x_v(5)
+        x_pe(6)
+        x_pe(7)
         w_quant(2)
         mx(1)
         exits(1)
-        x_pe(6)
         w_quant(3)
         x_v(6)
-        x_pe(7)
         x_v(7)
+        x_pe(8)
         mx(2)
         exits(2)
-        x_q(4)
-        x_q(5)
-        x_pe(8)
         x_v(8)
-        x_q(6)
-        x_q(7)
+        x_q(1)
         mx(3)
         exits(3)
         x_pe(9)
         x_v(9)
         spread_gb()
         x_pe(10)
-        x_v(10)
-        x_q(8)
-        x_q(9)
 
         h_pe(0)
-        for t in range(4, NT + 6):
-            i = t - 4
+        mx(4)
+        bn(0, 0)
+        for i in range(NT + 2):
             n = AHEAD + i
-            if t < NT:
-                mx(t)
-                exits(t)
-            if n < 4 * NB:
-                x_pe(n)
+            if 4 + i < NT:
+                exits(4 + i)
             if i + 1 < NT:
                 h_pe(i + 1)
-            if i < NT:
-                bn(i, 0)
-            if 0 <= i - 1 < LATE:
-                if post_kind(i - 1) == "G":
-                    nmr_v(i - 1)
-                scale_s(i - 1)
+                if half_on_scalar(i + 1):
+                    bn_s(i + 1)
+            if n + 1 < 4 * NB:
+                x_pe(n + 1)
+            if 5 + i < NT:
+                mx(5 + i)
             if i < NT:
                 bn(i, 1)
+            if 0 <= i - 1 < NT:
+                stt(i - 1, 1)
+                scale_s(i - 1)
             if n < 4 * NB:
                 x_v(n)
-            if i - 1 >= LATE and i - 1 < NT:
-                stt(i - 1)
             if i < NT:
                 aggr(i)
                 rs_s(i)
-            if n - 1 < 4 * NB:
-                x_q(n - 1)
-            if i < LATE and post_kind(i) != "G":
-                stt(i)
-            if 0 <= i - 1 < LATE:
+                if post_kind(i) == "G":
+                    nmr_s(i)
+            if i + 1 < NT:
+                bn(i + 1, 0)
+            if i < NT:
+                stt(i, 0)
+            if n < 4 * NB and n % 4 == 3:
+                x_q(n // 4)
+            if 0 <= i - 1 < NT:
                 fin(i - 1)
-            if i - 2 >= LATE and i - 2 < NT:
-                scale_s(i - 2)
-                fin(i - 2)

@@ -26,14 +26,12 @@ AHEAD = 10
 
 
 def half_on_scalar(i):
-    return False
+    return i % 2 == 0 and i > 0
 
 
 def post_kind(i):
     if i >= NT - 2:
         return "V"
-    if i < 20 and i % 3 == 1:
-        return "G"
     return "S"
 
 
@@ -54,10 +52,7 @@ def tile_onebitlinear_t_kernel(
         ypool = ctx.enter_context(tc.tile_pool(name="ypool", bufs=8))
         small = ctx.enter_context(tc.tile_pool(name="small", bufs=6))
         jpool = ctx.enter_context(tc.tile_pool(name="jpool", bufs=2))
-        psum_x = ctx.enter_context(tc.psum_pool(name="psum_x", bufs=2))
-        psum_m = ctx.enter_context(tc.psum_pool(name="psum_m", bufs=2))
-        psum_h = ctx.enter_context(tc.psum_pool(name="psum_h", bufs=4))
-        ctx.enter_context(tc.manual_schedule())
+        psum = ctx.enter_context(tc.psum_pool(name="psum", bufs=8))
 
         x_sb = {}
         xg = {}
@@ -125,26 +120,26 @@ def tile_onebitlinear_t_kernel(
             load_x(b)
 
         def spread_ics():
-            pt = psum_h.tile([P, 512], F32, name="pt", tag="hb")
+            pt = psum.tile([P, 512], F32, name="pt", tag="bank")
             nc.tensor.transpose(pt[:, 0:P], vrow[:], ident[:])
             nc.vector.tensor_copy(out=ics_w[:], in_=pt[:, 0:4])
 
         def spread_sb():
             nc.vector.tensor_copy(out=sbf[:], in_=sb16[:])
-            pt = psum_h.tile([P, 512], F32, name="pt", tag="hb")
+            pt = psum.tile([P, 512], F32, name="pt", tag="bank")
             nc.tensor.transpose(pt[:, 0:P], sbf[:], ident[:])
             nc.vector.tensor_copy(out=sb_t[:], in_=pt[:, 0:16])
 
         def spread_gb():
             for v in range(2):
-                pt = psum_h.tile([P, DO], BF16, name="ptb", tag="hb")
+                pt = psum.tile([P, DO], BF16, name="ptb", tag="bank")
                 for hn in range(2):
                     cols = slice(hn * 512, (hn + 1) * 512)
                     nc.tensor.matmul(pt[:, cols], lhsT=ones[:], rhs=gz[:, v, cols], start=True, stop=True)
                 nc.scalar.copy(out=gb16[:, v, :], in_=pt[:])
 
         def w_pe(j):
-            t = psum_h.tile([P, 512], F32, name="wt", tag="hb")
+            t = psum.tile([P, 512], F32, name="wt", tag="bank")
             for a in range(4):
                 nc.tensor.transpose(
                     t[:, a * P : (a + 1) * P], w_sb[:, j, :].bitcast(F32)[:, a * P : (a + 1) * P], ident[:]
@@ -192,7 +187,7 @@ def tile_onebitlinear_t_kernel(
         def x_pe(n):
             b, q = divmod(n, 4)
             hh, g = divmod(q, 2)
-            t = psum_x.tile([P, 512], F32, name="xtb", tag="xtb")
+            t = psum.tile([P, 512], F32, name="xtb", tag="bank")
             for u in range(2):
                 for cc in range(2):
                     k0 = (2 * g + u) * P
@@ -235,7 +230,7 @@ def tile_onebitlinear_t_kernel(
         def mx(t):
             b, q = divmod(t, 4)
             for j in (2 * q, 2 * q + 1):
-                acc = psum_m.tile([P, RB], F32, name="acc")
+                acc = psum.tile([P, RB], F32, name="acc", tag="bank")
                 accs[(b, j)] = acc
                 for g in range(2):
                     nc.tensor.matmul_mx(
@@ -265,7 +260,7 @@ def tile_onebitlinear_t_kernel(
         def h_pe(i, hns=(0, 1)):
             b, c = divmod(i, 4)
             for hn in hns:
-                t = psum_h.tile([P, 512], F32, name="htb", tag="hb")
+                t = psum.tile([P, 512], F32, name="htb", tag="bank")
                 for jj in range(4):
                     nc.tensor.transpose(
                         t[:, jj * P : (jj + 1) * P],

@@ -54,6 +54,8 @@ def tile_onebitlinear_t_kernel(
         jpool = ctx.enter_context(tc.tile_pool(name="jpool", bufs=2))
         psum = ctx.enter_context(tc.psum_pool(name="psum", bufs=8))
 
+        ctx.enter_context(tc.manual_schedule(engines={mybir.EngineType.PE}))
+
         x_sb = {}
         xg = {}
         xq = {}

@@ -45,13 +45,13 @@ def tile_onebitlinear_t_kernel(
 
     with ExitStack() as ctx:
         const = ctx.enter_context(tc.tile_pool(name="const", bufs=1))
-        xpool = ctx.enter_context(tc.tile_pool(name="xpool", bufs=NB))
+        xpool = ctx.enter_context(tc.tile_pool(name="xpool", bufs=5))
         gpool = ctx.enter_context(tc.tile_pool(name="gpool", bufs=3))
-        qpool = ctx.enter_context(tc.tile_pool(name="qpool", bufs=4))
-        hpool = ctx.enter_context(tc.tile_pool(name="hpool", bufs=2))
+        qpool = ctx.enter_context(tc.tile_pool(name="qpool", bufs=5))
+        hpool = ctx.enter_context(tc.tile_pool(name="hpool", bufs=3))
         ypool = ctx.enter_context(tc.tile_pool(name="ypool", bufs=8))
-        small = ctx.enter_context(tc.tile_pool(name="small", bufs=6))
-        jpool = ctx.enter_context(tc.tile_pool(name="jpool", bufs=2))
+        small = ctx.enter_context(tc.tile_pool(name="small", bufs=8))
+        jpool = ctx.enter_context(tc.tile_pool(name="jpool", bufs=4))
         psum = ctx.enter_context(tc.psum_pool(name="psum", bufs=8))
 
         ctx.enter_context(tc.manual_schedule(engines={mybir.EngineType.PE}))

@@ -32,6 +32,8 @@ def half_on_scalar(i):
 def post_kind(i):
     if i >= NT - 2:
         return "V"
+    if i % 4 == 1 and i < 24:
+        return "GS"
     return "S"
 
 
@@ -350,17 +352,6 @@ def tile_onebitlinear_t_kernel(
             if kind == "S":
                 y = yt[i]
                 nc.scalar.activation(out=y[:], in_=y[:], func=ACT.Copy, scale=rstds[i][:, 0:1])
-            elif kind == "G":
-                y = ypool.tile([P, DO], F32, name="y")
-                yt[i] = y
-                for hn in range(2):
-                    nc.scalar.activation(
-                        out=y[:, hn * 512 : (hn + 1) * 512],
-                        in_=ht[(i, hn)][:],
-                        func=ACT.Identity,
-                        bias=nmrs[i][:, 0:1],
-                        scale=rstds[i][:, 0:1],
-                    )
 
         def fin(i):
             b, c = divmod(i, 4)
@@ -379,8 +370,10 @@ def tile_onebitlinear_t_kernel(
                     )
                     nc.sync.dma_start(out=o_blk[b, c][:, cols], in_=y[:, cols])
                 return
-            if kind == "G":
-                nc.gpsimd.tensor_tensor(out=y[:], in0=y[:], in1=gb16[:, 0, :], op=ALU.mult)
+            if kind == "GS":
+                nc.gpsimd.tensor_scalar(
+                    out=y[:], in0=y[:], scalar1=rstds[i][:, 0:1], scalar2=0.0, op0=ALU.mult, op1=ALU.add
+                )
             nc.gpsimd.tensor_tensor(out=y[:], in0=y[:], in1=gb16[:, 1, :], op=ALU.add)
             nc.sync.dma_start(out=o_blk[b, c], in_=y[:])
 

from contextlib import ExitStack

import concourse.mybir as mybir
from concourse.masks import make_identity

F32 = mybir.dt.float32
BF16 = mybir.dt.bfloat16
U32 = mybir.dt.uint32
U8 = mybir.dt.uint8
FP8X4 = mybir.dt.float8_e4m3fn_x4
ALU = mybir.AluOpType
ACT = mybir.ActivationFunctionType

P = 128
R = 4096
DI = 1024
DO = 1024
RB = 512
NB = R // RB
NT = R // P
NJ = DO // P
LN_EPS = 1e-5
FLOPS = 2 * R * DI * DO

AHEAD = 10


def half_on_scalar(i):
    return i % 2 == 0 and i > 0


def post_kind(i):
    if i >= NT - 2:
        return "V"
    if i % 4 == 1 and i < 24:
        return "GS"
    return "S"


def tile_onebitlinear_t_kernel(
    tc, x, weight, in_channel_scale, out_channel_scale, bias, ln_gamma, ln_beta, out
):
    nc = tc.nc
    x_blk = x.flatten_outer_dims().rearrange("(i p c) k -> i p c k", p=P, c=4)
    w_v = weight.rearrange("(j p) k -> p j k", p=P)
    o_blk = out.flatten_outer_dims().rearrange("(i p c) n -> i c p n", p=P, c=4)

    with ExitStack() as ctx:
        const = ctx.enter_context(tc.tile_pool(name="const", bufs=1))
        xpool = ctx.enter_context(tc.tile_pool(name="xpool", bufs=5))
        gpool = ctx.enter_context(tc.tile_pool(name="gpool", bufs=3))
        qpool = ctx.enter_context(tc.tile_pool(name="qpool", bufs=5))
        hpool = ctx.enter_context(tc.tile_pool(name="hpool", bufs=3))
        ypool = ctx.enter_context(tc.tile_pool(name="ypool", bufs=8))
        small = ctx.enter_context(tc.tile_pool(name="small", bufs=8))
        jpool = ctx.enter_context(tc.tile_pool(name="jpool", bufs=4))
        psum = ctx.enter_context(tc.psum_pool(name="psum", bufs=8))

        ctx.enter_context(tc.manual_schedule(engines={mybir.EngineType.PE}))

        x_sb = {}
        xg = {}
        xq = {}
        xsc = {}
        xt = {}
        wt = {}
        hT = {}
        ht = {}
        yt = {}
        mvs = {}
        rstds = {}
        nmrs = {}

        def load_x(b):
            xs = xpool.tile([P, 4, DI], BF16, name="xs")
            x_sb[b] = xs
            if b == 0:
                nc.sync.dma_start(out=xs[:, 0:2, :], in_=x_blk[b][:, 0:2, :])
                load_w(0)
                nc.sync.dma_start(out=xs[:, 2:4, :], in_=x_blk[b][:, 2:4, :])
            else:
                nc.sync.dma_start(out=xs[:], in_=x_blk[b])

        ident = const.tile([P, P], F32, name="ident")
        make_identity(nc, ident[:])
        vrow = const.tile([P, P], F32, name="vrow")
        nc.vector.memset(vrow[:], 0.0)
        sb16 = const.tile([P, P], BF16, name="sb16")
        nc.vector.memset(sb16[:], 0.0)
        gz = const.tile([P, 2, DO], BF16, name="gz")
        nc.vector.memset(gz[:], 0.0)
        ones = const.tile([P, P], BF16, name="ones")
        nc.vector.memset(ones[:], 1.0)
        eps_t = const.tile([P, 1], F32, name="eps_t")
        nc.vector.memset(eps_t[:], LN_EPS)
        sgn_b = const.tile([P, 1], F32, name="sgn_b")
        nc.vector.memset(sgn_b[:], 2.0 ** -80)
        nc.scalar.dma_start(
            out=vrow[0:4, :].bitcast(BF16), in_=in_channel_scale.rearrange("(a k) -> a k", a=4)
        )
        nc.scalar.dma_start(out=sb16[0:8, :], in_=out_channel_scale.rearrange("(j p) -> j p", p=P))
        nc.scalar.dma_start(out=sb16[8:16, :], in_=bias.rearrange("(j p) -> j p", p=P))
        nc.scalar.dma_start(out=gz[0:1, 0, :], in_=ln_gamma.rearrange("(o n) -> o n", o=1))
        nc.scalar.dma_start(out=gz[0:1, 1, :], in_=ln_beta.rearrange("(o n) -> o n", o=1))
        ics_w = const.tile([P, 4], F32, name="ics_w")
        ics_t = ics_w[:].bitcast(BF16)
        sbf = const.tile([P, P], F32, name="sbf")
        sb_t = const.tile([P, 16], F32, name="sb_t")
        s_t = sb_t[:, 0:NJ]
        b_t = sb_t[:, NJ : 2 * NJ]
        gb16 = const.tile([P, 2, DO], BF16, name="gb16")
        w_sb = const.tile([P, NJ, DI], BF16, name="w_sb")
        wg = const.tile([P, 2, DO, 4], BF16, name="wg", align_bytes=64)
        wq = const.tile([P, 2, DO], U32, name="wq", align_bytes=64)
        wsc = const.tile([P, 2, DO], U8, name="wsc", align_bytes=64)

        def load_w(q):
            nc.sync.dma_start(out=w_sb[:, 2 * q : 2 * q + 2], in_=w_v[:, 2 * q : 2 * q + 2])

        load_x(0)
        for q in range(1, 4):
            load_w(q)
        for b in range(1, NB):
            load_x(b)

        def spread_ics():
            pt = psum.tile([P, 512], F32, name="pt", tag="bank")
            nc.tensor.transpose(pt[:, 0:P], vrow[:], ident[:])
            nc.vector.tensor_copy(out=ics_w[:], in_=pt[:, 0:4])

        def spread_sb():
            nc.vector.tensor_copy(out=sbf[:], in_=sb16[:])
            pt = psum.tile([P, 512], F32, name="pt", tag="bank")
            nc.tensor.transpose(pt[:, 0:P], sbf[:], ident[:])
            nc.vector.tensor_copy(out=sb_t[:], in_=pt[:, 0:16])

        def spread_gb():
            for v in range(2):
                pt = psum.tile([P, DO], BF16, name="ptb", tag="bank")
                for hn in range(2):
                    cols = slice(hn * 512, (hn + 1) * 512)
                    nc.tensor.matmul(pt[:, cols], lhsT=ones[:], rhs=gz[:, v, cols], start=True, stop=True)
                nc.scalar.copy(out=gb16[:, v, :], in_=pt[:])

        def w_pe(j):
            t = psum.tile([P, 512], F32, name="wt", tag="bank")
            for a in range(4):
                nc.tensor.transpose(
                    t[:, a * P : (a + 1) * P], w_sb[:, j, :].bitcast(F32)[:, a * P : (a + 1) * P], ident[:]
                )
            wt[j] = t

        def w_sign(j):
            wv = wt[j][:].bitcast(BF16)
            for g in range(2):
                nc.scalar.activation(
                    out=wg[:, g, j * P : (j + 1) * P, :].rearrange("p n (u e) -> p n u e", u=2),
                    in_=wv[:, g * 512 : (g + 1) * 512].rearrange("p (u n e) -> p n u e", u=2, e=2),
                    func=ACT.Sign,
                    bias=sgn_b[:, 0:1],
                    scale=2.0 ** 64,
                )

        def w_ge(q):
            wv = w_sb[:, 2 * q : 2 * q + 2, :].rearrange("p j k -> p (j k)")
            nc.vector.tensor_scalar(out=wv, in0=wv, scalar1=0.0, scalar2=2.0, op0=ALU.is_ge, op1=ALU.mult)

        def w_pm(q):
            wv = w_sb[:, 2 * q : 2 * q + 2, :].rearrange("p j k -> p (j k)")
            nc.vector.tensor_scalar(out=wv, in0=wv, scalar1=1.0, scalar2=-1.0, op0=ALU.mult, op1=ALU.add)

        def w_copy(j):
            for g in range(2):
                nc.scalar.copy(
                    out=wg[:, g, j * P : (j + 1) * P, :]
                    .rearrange("p n t -> p (n t)")
                    .bitcast(F32)
                    .rearrange("p (n u) -> p n u", u=2),
                    in_=wt[j][:, g * 256 : (g + 1) * 256].rearrange("p (u n) -> p n u", u=2),
                )

        def w_quant(q):
            cols = slice(256 * q, 256 * (q + 1))
            for g in range(2):
                nc.vector.quantize_mx(
                    out=wq[:, g, cols].bitcast(FP8X4),
                    scales=wsc[:, g, cols],
                    in_=wg[:, g, cols, :].rearrange("p n t -> p (n t)"),
                )

        def x_pe(n):
            b, q = divmod(n, 4)
            hh, g = divmod(q, 2)
            t = psum.tile([P, 512], F32, name="xtb", tag="bank")
            for u in range(2):
                for cc in range(2):
                    k0 = (2 * g + u) * P
                    nc.tensor.transpose(
                        t[:, (2 * u + cc) * P : (2 * u + cc + 1) * P],
                        x_sb[b][:, 2 * hh + cc, :].bitcast(F32)[:, k0 : k0 + P],
                        ident[:],
                    )
            xt[n] = t

        def x_v(n):
            b, q = divmod(n, 4)
            hh, g = divmod(q, 2)
            if q == 0:
                xgt = gpool.tile([P, 2, RB, 4], BF16, name="xgt", align_bytes=64)
                xg[b] = xgt
            nc.vector.tensor_tensor(
                out=xg[b][:, g, hh * 256 : (hh + 1) * 256, :].rearrange("p m (u e) -> p m u e", u=2),
                in0=xt[n][:].bitcast(BF16).rearrange("p (u m e) -> p m u e", u=2, e=2),
                in1=ics_t[:, 4 * g : 4 * g + 4]
                .rearrange("p (u e) -> p u e", u=2)
                .unsqueeze(1)
                .to_broadcast([P, 256, 2, 2]),
                op=ALU.mult,
            )

        def x_q(b):
            xqt = qpool.tile([P, 2, RB], U32, name="xqt", align_bytes=64)
            xst = qpool.tile([P, 2, RB], U8, name="xst", align_bytes=64)
            xq[b] = xqt
            xsc[b] = xst
            nc.vector.quantize_mx(
                out=xqt[:].rearrange("p g m -> p (g m)").bitcast(FP8X4),
                scales=xst[:].rearrange("p g m -> p (g m)"),
                in_=xg[b][:].rearrange("p g m t -> p (g m t)"),
            )

        accs = {}

        def mx(t):
            b, q = divmod(t, 4)
            for j in (2 * q, 2 * q + 1):
                acc = psum.tile([P, RB], F32, name="acc", tag="bank")
                accs[(b, j)] = acc
                for g in range(2):
                    nc.tensor.matmul_mx(
                        out=acc[:],
                        lhsT=wq[:, g, j * P : (j + 1) * P].bitcast(FP8X4),
                        lhsT_scale=wsc[:, g, j * P : (j + 1) * P],
                        rhs=xq[b][:, g, :].bitcast(FP8X4),
                        rhs_scale=xsc[b][:, g, :],
                        start=(g == 0),
                        stop=(g == 1),
                    )

        def exits(t):
            b, q = divmod(t, 4)
            if q == 0:
                hTt = hpool.tile([P, NJ, RB], F32, name="hTt")
                hT[b] = hTt
            for j in (2 * q, 2 * q + 1):
                nc.scalar.activation(
                    out=hT[b][:, j, :],
                    in_=accs[(b, j)][:],
                    func=ACT.Identity,
                    bias=b_t[:, j : j + 1],
                    scale=s_t[:, j : j + 1],
                )

        def h_pe(i, hns=(0, 1)):
            b, c = divmod(i, 4)
            for hn in hns:
                t = psum.tile([P, 512], F32, name="htb", tag="bank")
                for jj in range(4):
                    nc.tensor.transpose(
                        t[:, jj * P : (jj + 1) * P],
                        hT[b][:, 4 * hn + jj, c * P : (c + 1) * P],
                        ident[:],
                    )
                ht[(i, hn)] = t

        sts = {}

        sth = []
        for n in range(4):
            st = const.tile([P, 9], F32, name=f"sth{n}")
            nc.gpsimd.memset(st[:], 512.0)
            sth.append(st)

        def bn(i, hn):
            if hn == 0:
                if half_on_scalar(i):
                    st = sth[i % 4]
                else:
                    st = small.tile([P, 12], F32, name="st")
                sts[i] = st
            elif half_on_scalar(i):
                return
            nc.vector.bn_stats(out=sts[i][:, 6 * hn : 6 * hn + 6], in_=ht[(i, hn)][:])

        def bn_s(i):
            st = sth[i % 4]
            junk = jpool.tile([P, 512], BF16, name="junk")
            nc.scalar.activation(
                out=junk[:], in_=ht[(i, 1)][:], func=ACT.Identity, scale=1.0 / 512, accum_out=st[:, 7:8]
            )
            junk = jpool.tile([P, 512], BF16, name="junk")
            nc.scalar.activation(
                out=junk[:],
                in_=ht[(i, 1)][:],
                func=ACT.Square,
                bias=st[:, 7:8],
                scale=-1.0,
                accum_out=st[:, 8:9],
            )

        def aggr(i):
            mv = small.tile([P, 2], F32, name="mv")
            nc.vector.bn_aggr(out=mv[:], in_=sts[i][:, 0 : 9 if half_on_scalar(i) else 12])
            mvs[i] = mv

        def stt(i, hn):
            if post_kind(i) == "G":
                return
            if hn == 0:
                y = ypool.tile([P, DO], F32, name="y")
                yt[i] = y
            cols = slice(hn * 512, (hn + 1) * 512)
            nc.vector.scalar_tensor_tensor(
                out=yt[i][:, cols],
                in0=ht[(i, hn)][:],
                scalar=mvs[i][:, 0:1],
                in1=gb16[:, 0, cols],
                op0=ALU.subtract,
                op1=ALU.mult,
            )

        def rs_s(i):
            rs = small.tile([P, 1], F32, name="rs")
            nc.scalar.activation(
                out=rs[:],
                in_=mvs[i][:, 1:2],
                func=ACT.Abs_reciprocal_sqrt,
                bias=eps_t[:, 0:1],
                scale=1.0,
            )
            rstds[i] = rs

        def nmr_s(i):
            nrs = small.tile([P, 1], F32, name="nrs")
            nc.scalar.activation(out=nrs[:], in_=rstds[i][:], func=ACT.Copy, scale=-1.0)
            nmr = small.tile([P, 1], F32, name="nmr")
            nc.scalar.activation(out=nmr[:], in_=mvs[i][:, 0:1], func=ACT.Copy, scale=nrs[:, 0:1])
            nmrs[i] = nmr

        def scale_s(i):
            kind = post_kind(i)
            if kind == "S":
                y = yt[i]
                nc.scalar.activation(out=y[:], in_=y[:], func=ACT.Copy, scale=rstds[i][:, 0:1])

        def fin(i):
            b, c = divmod(i, 4)
            kind = post_kind(i)
            y = yt[i]
            if kind == "V":
                for hn in range(2):
                    cols = slice(hn * 512, (hn + 1) * 512)
                    nc.vector.scalar_tensor_tensor(
                        out=y[:, cols],
                        in0=y[:, cols],
                        scalar=rstds[i][:, 0:1],
                        in1=gb16[:, 1, cols],
                        op0=ALU.mult,
                        op1=ALU.add,
                    )
                    nc.sync.dma_start(out=o_blk[b, c][:, cols], in_=y[:, cols])
                return
            if kind == "GS":
                nc.gpsimd.tensor_scalar(
                    out=y[:], in0=y[:], scalar1=rstds[i][:, 0:1], scalar2=0.0, op0=ALU.mult, op1=ALU.add
                )
            nc.gpsimd.tensor_tensor(out=y[:], in0=y[:], in1=gb16[:, 1, :], op=ALU.add)
            nc.sync.dma_start(out=o_blk[b, c], in_=y[:])

        spread_ics()
        for n in range(2):
            x_pe(n)
            x_v(n)
        for j in range(2):
            w_pe(j)
            w_sign(j)
        for n in range(2, 4):
            x_pe(n)
            x_v(n)
        for j in range(2, 4):
            w_pe(j)
            w_sign(j)
        spread_sb()
        w_ge(2)
        w_ge(3)
        w_pm(2)
        x_q(0)
        w_pm(3)
        for j in (4, 5):
            w_pe(j)
            w_copy(j)
        w_quant(0)
        x_pe(4)
        x_pe(5)
        for j in (6, 7):
            w_pe(j)
            w_copy(j)
        mx(0)
        exits(0)
        w_quant(1)
        x_v(4)
        x_v(5)
        x_pe(6)
        x_pe(7)
        w_quant(2)
        mx(1)
        exits(1)
        w_quant(3)
        x_v(6)
        x_v(7)
        x_pe(8)
        mx(2)
        exits(2)
        x_v(8)
        x_q(1)
        mx(3)
        exits(3)
        x_pe(9)
        x_v(9)
        spread_gb()
        x_pe(10)

        h_pe(0)
        mx(4)
        bn(0, 0)
        for i in range(NT + 2):
            n = AHEAD + i
            if 4 + i < NT:
                exits(4 + i)
            if i + 1 < NT:
                h_pe(i + 1)
                if half_on_scalar(i + 1):
                    bn_s(i + 1)
            if n + 1 < 4 * NB:
                x_pe(n + 1)
            if 5 + i < NT:
                mx(5 + i)
            if i < NT:
                bn(i, 1)
            if 0 <= i - 1 < NT:
                stt(i - 1, 1)
                scale_s(i - 1)
            if n < 4 * NB:
                x_v(n)
            if i < NT:
                aggr(i)
                rs_s(i)
                if post_kind(i) == "G":
                    nmr_s(i)
            if i + 1 < NT:
                bn(i + 1, 0)
            if i < NT:
                stt(i, 0)
            if n < 4 * NB and n % 4 == 3:
                x_q(n // 4)
            if 0 <= i - 1 < NT:
                fin(i - 1)
